import numpy as np
import ml_dtypes


def mxq(x, axis, fmt="e4m3"):
    dtype, down = {"e4m3": (ml_dtypes.float8_e4m3fn, 7), "e5m2": (ml_dtypes.float8_e5m2, 14)}[fmt]
    v = np.moveaxis(np.asarray(x, np.float32).astype(ml_dtypes.bfloat16).astype(np.float64), axis, -1)
    blocks = v.reshape(v.shape[:-1] + (-1, 32))
    amax = np.abs(blocks).max(-1, keepdims=True)
    byte = np.maximum(np.where(amax > 0, np.frexp(amax)[1] - 1 + 127, 0) - down, 1)
    scale = np.exp2(byte - 127.0)
    codes = (blocks / scale).astype(np.float32).astype(dtype).astype(np.float64)
    return np.moveaxis((codes * scale).reshape(v.shape), -1, axis)


WIDE = False


def mx_kscale(k):
    if not WIDE:
        return np.ones(k)
    levels = np.array([10, -10, 5, -5, 0])
    if k % 512:
        return np.exp2(np.random.permutation(np.resize(levels, k // 32))).repeat(32)
    a = np.empty((k // 512, 16))
    for p in range(k // 512):
        a[p, :8] = np.random.permutation(np.resize(levels, 8))
        for g in range(8):
            far = levels[np.abs(levels - a[p, g]) >= 10]
            a[p, g + 8] = far[np.random.randint(len(far))]
    return np.exp2(a.ravel()).repeat(32)


BF16 = ml_dtypes.bfloat16


def bf(x):
    return np.asarray(x, np.float32).astype(BF16)


def f64(x):
    return np.asarray(x).astype(np.float64)


B, D0, D1, D2, D3 = 4096, 1024, 512, 512, 2048
HEBB = 0.01
RATE = 0.001
BATCH_NUM = 1
C = HEBB * RATE / BATCH_NUM


def centred(s):
    return s / np.exp2(np.round(np.log2(s.mean())))


def setup_inputs():
    s, t = centred(mx_kscale(D0)), centred(mx_kscale(D1))
    return {"x": bf((4.0 + 3.0 * np.random.standard_normal((B, D0))) * s),
            "W1": bf(np.random.standard_normal((D1, D0)) * 0.9 / np.sqrt(D0) / s[None, :] * t[:, None]),
            "b1": bf((3.0 + 1.5 * np.random.standard_normal(D1)) * t),
            "W2": bf(np.random.standard_normal((D2, D1)) * 0.9 / np.sqrt(D1) / t[None, :]),
            "b2": bf(3.0 + 1.5 * np.random.standard_normal(D2))}


def reference(x, W1, b1, W2, b2):
    x = f64(x)
    v1 = np.maximum((mxq(x, 1, "e4m3") @ mxq(f64(W1), 1, "e4m3").T) + f64(b1), 0.0)
    m1 = np.mean(v1, axis=0)
    h = v1 + np.sum(x, axis=1, keepdims=True) * (C * m1)[None, :]
    v2 = np.maximum((mxq(h, 1, "e4m3") @ mxq(f64(W2), 1, "e4m3").T) + f64(b2), 0.0)
    m2 = np.mean(v2, axis=0)
    out = v2 + np.sum(h, axis=1, keepdims=True) * (C * m2)[None, :]
    return out, m1, m2

@@ -1,0 +1,422 @@
+from contextlib import ExitStack
+
+import concourse.mybir as mybir
+from concourse.masks import make_identity
+
+F32 = mybir.dt.float32
+BF16 = mybir.dt.bfloat16
+U32 = mybir.dt.uint32
+U8 = mybir.dt.uint8
+FP8X4 = mybir.dt.float8_e4m3fn_x4
+ALU = mybir.AluOpType
+FN = mybir.ActivationFunctionType
+AXIS = mybir.AxisListType
+
+P = 128
+ROWS, D0, D1, D2 = 4096, 1024, 512, 512
+C = 0.01 * 0.001 / 1
+NT = ROWS // P
+CH = 8
+CW = 512
+FLOPS = 2 * ROWS * D0 * D1 + 2 * ROWS * D1 * D2
+
+
+def tile_optimalnet_pa_t_kernel(tc, x, W1, b1, W2, b2, out_0, out_1, out_2):
+    nc = tc.nc
+    x_v = x.rearrange("(p a) i -> p (a i)", a=NT)
+    out_v = out_0.rearrange("(p a) o -> p (a o)", a=NT)
+
+    with ExitStack() as ctx:
+        ctx.enter_context(tc.manual_schedule())
+        keep = ctx.enter_context(tc.tile_pool(name="keep", bufs=1))
+        pt = ctx.enter_context(tc.psum_pool(name="pt", bufs=4))
+        pz = ctx.enter_context(tc.psum_pool(name="pz", bufs=4))
+
+        ht = {}
+        hv = [keep.tile([P, 4 * CW], F32, name="hv%d" % c) for c in range(CH)]
+        xq = [keep.tile([P, 2 * CW], U32, name="xq%d" % c, align_bytes=64) for c in range(CH)]
+        sacc = [keep.tile([P, CW], F32, name="sacc%d" % c) for c in range(CH)]
+        xs = [keep.tile([P, 2 * CW], U8, name="xs%d" % c, align_bytes=64) for c in range(CH)]
+        w1q = keep.tile([P, 1024], U32, name="w1q", align_bytes=64)
+        w1s = keep.tile([P, 1024], U8, name="w1s", align_bytes=64)
+        w2q = keep.tile([P, 512], U32, name="w2q", align_bytes=64)
+        w2s = keep.tile([P, 512], U8, name="w2s", align_bytes=64)
+        ident = keep.tile([P, P], F32, name="ident")
+        b1f = keep.tile([P, 4], F32, name="b1f")
+        b2f = keep.tile([P, 4], F32, name="b2f")
+        acc1 = keep.tile([P, 32], F32, name="acc1")
+        acc2 = keep.tile([P, 32], F32, name="acc2")
+        sx = keep.tile([P, NT], F32, name="sx")
+        sxa = keep.tile([P, CH], F32, name="sxa")
+        jxa = keep.tile([P, D0], BF16, name="jxa")
+        sh = keep.tile([P, NT], F32, name="sh")
+        sv = keep.tile([P, NT], F32, name="sv")
+        k1 = keep.tile([P, 1], F32, name="k1")
+        cm1 = keep.tile([P, 4], F32, name="cm1")
+        s1 = keep.tile([P, 4], F32, name="s1")
+        s2 = keep.tile([P, 4], F32, name="s2")
+        jx = keep.tile([P, D0], BF16, name="jx")
+        ja = keep.tile([P, CW], BF16, name="ja")
+        j8 = keep.tile([P, 8], F32, name="j8")
+        cm2b = keep.tile([P, D2], F32, name="cm2b")
+        m2r = keep.tile([P, D2], F32, name="m2r")
+        m1r = keep.tile([P, D1], F32, name="m1r")
+
+        make_identity(nc, ident[:])
+
+        def four_transposes(bank, words, first):
+            for b in range(4):
+                g, u = b // 2, b % 2
+                w0 = first + g * 2 * P + u
+                nc.tensor.transpose(bank[:, b * P : (b + 1) * P], words[:, w0 : first + (g + 1) * 2 * P : 2], ident[:])
+
+        def exit_words(grouped, col0, bank):
+            dst = grouped[:].bitcast(F32).rearrange("q (g c u) -> q g c u", g=2, u=2)
+            nc.scalar.copy(
+                out=dst[:, :, col0 : col0 + P, :],
+                in_=bank[:].rearrange("q (g u c) -> q g c u", g=2, u=2),
+            )
+
+        def layer1(t, c):
+            z = pz.tile([P, CW], F32, name="z", tag="z")
+            for g in range(2):
+                wcols = slice(g * 512 + t * P, g * 512 + (t + 1) * P)
+                xcols = slice(g * CW, (g + 1) * CW)
+                nc.tensor.matmul_mx(
+                    out=z[:],
+                    lhsT=w1q[:, wcols].bitcast(FP8X4),
+                    lhsT_scale=w1s[:, wcols],
+                    rhs=xq[c][:, xcols].bitcast(FP8X4),
+                    rhs_scale=xs[c][:, xcols],
+                    start=(g == 0),
+                    stop=(g == 1),
+                )
+            nc.scalar.activation(
+                out=hv[c][:, t * CW : (t + 1) * CW],
+                in_=z[:],
+                func=FN.Relu,
+                bias=b1f[:, t : t + 1],
+                scale=1.0,
+                accum_out=acc1[:, t * CH + c : t * CH + c + 1],
+            )
+
+        def add_tiles_01(c):
+            nc.gpsimd.tensor_tensor(out=sacc[c][:], in0=hv[c][:, 0:CW], in1=hv[c][:, CW : 2 * CW], op=ALU.add)
+
+        def add_tile_2(c):
+            nc.gpsimd.tensor_tensor(out=sacc[c][:], in0=sacc[c][:], in1=hv[c][:, 2 * CW : 3 * CW], op=ALU.add)
+
+        def spread_row_sums(c):
+            sb = pt.tile([P, CW], F32, name="sb", tag="pt")
+            for l in range(4):
+                a = 4 * c + l
+                col = sxa[:, c : c + 1] if l == 3 else sx[:, a : a + 1]
+                nc.tensor.transpose(sb[:, l * P : (l + 1) * P], col.to_broadcast([P, P]), ident[:])
+            return sb
+
+        def scaled_mean1(t):
+            nc.vector.tensor_scalar(
+                out=j8[:],
+                in0=acc1[:, t * CH : (t + 1) * CH],
+                scalar1=C / ROWS,
+                scalar2=None,
+                op0=ALU.mult,
+                op1=ALU.add,
+                accum_out=cm1[:, t : t + 1],
+            )
+
+        def correct(t, c, sb):
+            seg = slice(t * CW, (t + 1) * CW)
+            nc.vector.scalar_tensor_tensor(
+                out=ht[c][:, seg], in0=sb[:], scalar=cm1[:, t : t + 1], in1=hv[c][:, seg], op0=ALU.mult, op1=ALU.add
+            )
+
+        def row_sums_v1(c, on_scalar):
+            bank = pz.tile([P, CW], F32, name="svb", tag="z")
+            for l in range(4):
+                parts = (sacc[c][:, l * P : (l + 1) * P], hv[c][:, 3 * CW + l * P : 3 * CW + (l + 1) * P])
+                for k in range(2):
+                    nc.tensor.matmul(
+                        out=bank[:, l * P : (l + 1) * P],
+                        lhsT=parts[k],
+                        rhs=ident[:],
+                        is_transpose=True,
+                        start=(k == 0),
+                        stop=(k == 1),
+                    )
+            if on_scalar:
+                for l in range(4):
+                    a = 4 * c + l
+                    nc.scalar.activation(
+                        out=ja[:, 0:P], in_=bank[:, l * P : (l + 1) * P], func=FN.Copy, accum_out=sv[:, a : a + 1]
+                    )
+            return bank
+
+        def reduce_row_sums(c, bank):
+            nc.vector.tensor_reduce(
+                out=sv[:, 4 * c : 4 * c + 4], in_=bank[:].rearrange("p (l k) -> p l k", l=4), axis=AXIS.X, op=ALU.add
+            )
+
+        with tc.tile_pool(name="stage", bufs=1) as stage:
+            xn = {}
+
+            def load_x(c):
+                xt = stage.tile([P, 4 * D0], BF16, name="xn", tag="xn", bufs=5)
+                nc.sync.dma_start(out=xt[:], in_=x_v[:, c * 4 * D0 : (c + 1) * 4 * D0])
+                xn[c] = xt
+
+            xg = {}
+
+            def transpose_x(c):
+                g_t = stage.tile([P, 4 * D0], BF16, name="xg", tag="xg", bufs=2, align_bytes=64)
+                xg[c] = g_t
+                words = xn[c][:].bitcast(F32)
+                for l in range(4):
+                    bank = pt.tile([P, CW], F32, name="xt", tag="pt")
+                    four_transposes(bank, words, l * 512)
+                    exit_words(g_t, l * P, bank)
+
+            def row_sums_x(c):
+                nc.scalar.activation(
+                    out=jxa[:], in_=xn[c][:, 3 * D0 : 4 * D0], func=FN.Copy, accum_out=sxa[:, c : c + 1]
+                )
+                for l in range(3):
+                    a = 4 * c + l
+                    nc.vector.tensor_scalar(
+                        out=jx[:],
+                        in0=xn[c][:, l * D0 : (l + 1) * D0],
+                        scalar1=1.0,
+                        scalar2=None,
+                        op0=ALU.mult,
+                        op1=ALU.add,
+                        accum_out=sx[:, a : a + 1],
+                    )
+
+            def quantise_x(c):
+                nc.vector.quantize_mx(out=xq[c][:].bitcast(FP8X4), scales=xs[c][:], in_=xg[c][:])
+
+            w1n = stage.tile([P, 4 * D0], BF16, name="w1n")
+            w1g = stage.tile([P, 4 * D0], BF16, name="w1g", align_bytes=64)
+            w2n = stage.tile([P, 4 * D1], BF16, name="w2n")
+            w2g = stage.tile([P, 4 * D1], BF16, name="w2g", align_bytes=64)
+            b1r = stage.tile([P, 4], BF16, name="b1r")
+            b2r = stage.tile([4, P], BF16, name="b2r")
+            b2pad = stage.tile([P, P], F32, name="b2pad")
+
+            first = stage.tile([P, 4 * D0], BF16, name="xn", tag="xn", bufs=5)
+            xn[0] = first
+            for l in range(4):
+                nc.sync.dma_start(out=first[:, l * D0 : (l + 1) * D0], in_=x_v[:, l * D0 : (l + 1) * D0])
+            nc.sync.dma_start(out=w1n[:], in_=W1.rearrange("(p t) i -> p (t i)", t=4))
+            load_x(1)
+            nc.sync.dma_start(
+                out=w2n[:].rearrange("p (t o) -> p t o", t=4), in_=W2.rearrange("(t p) o -> p t o", p=P)
+            )
+            for c in range(2, 5):
+                load_x(c)
+            nc.scalar.dma_start(out=b1r[:], in_=b1.rearrange("(p t) -> p t", t=4))
+            nc.scalar.dma_start(out=b2r[:], in_=b2.rearrange("(t p) -> t p", p=P))
+
+            nc.vector.memset(b2pad[:], 0.0)
+            nc.vector.tensor_copy(out=b1f[:], in_=b1r[:])
+            nc.vector.tensor_copy(out=b2pad[0:4, :], in_=b2r[:])
+
+            transpose_x(0)
+            row_sums_x(0)
+            w1words = w1n[:].bitcast(F32)
+            for t in range(4):
+                bank = pt.tile([P, CW], F32, name="w1t", tag="pt")
+                four_transposes(bank, w1words, t * 512)
+                exit_words(w1g, t * P, bank)
+            nc.vector.quantize_mx(out=w1q[:].bitcast(FP8X4), scales=w1s[:], in_=w1g[:])
+            transpose_x(1)
+            row_sums_x(1)
+            load_x(5)
+            load_x(6)
+
+            sbs = {}
+            for c in range(CH):
+                quantise_x(c)
+                if c + 2 < CH - 2:
+                    row_sums_x(c + 2)
+                if c >= CH - 2:
+                    row_sums_x(c)
+                layer1(0, c)
+                if c + 2 < CH:
+                    transpose_x(c + 2)
+                if c == CH - 1:
+                    for cc in range(4):
+                        sbs[cc] = spread_row_sums(cc)
+                layer1(1, c)
+                add_tiles_01(c)
+                if c == 0:
+                    load_x(7)
+                if c == 2:
+                    w2words = w2n[:].bitcast(F32).rearrange("p (t w u) -> p t u w", t=4, u=2)
+                    w2gw = w2g[:].bitcast(F32).rearrange("q (t c u) -> q t c u", t=4, u=2)
+                    for h in range(2):
+                        bank = pt.tile([P, CW], F32, name="w2t", tag="pt")
+                        for tl in range(2):
+                            for u in range(2):
+                                k = tl * 2 + u
+                                nc.tensor.transpose(
+                                    bank[:, k * P : (k + 1) * P], w2words[:, 2 * h + tl, u, :], ident[:]
+                                )
+                        nc.scalar.copy(
+                            out=w2gw[:, 2 * h : 2 * h + 2, :, :],
+                            in_=bank[:].rearrange("q (t u c) -> q t c u", t=2, u=2),
+                        )
+                    bank = pt.tile([P, CW], F32, name="b2t", tag="pt")
+                    nc.tensor.transpose(bank[:, 0:P], b2pad[:], ident[:])
+                    nc.scalar.copy(out=b2f[:], in_=bank[:, 0:4])
+                if c == 3:
+                    nc.vector.quantize_mx(out=w2q[:].bitcast(FP8X4), scales=w2s[:], in_=w2g[:])
+
+        work = ctx.enter_context(tc.tile_pool(name="work", bufs=1))
+        for c in range(CH):
+            ht[c] = work.tile([P, 4 * CW], BF16, name="ht%d" % c)
+        v2 = {}
+
+        scaled_mean1(0)
+        scaled_mean1(1)
+        for n in range(16):
+            layer1(2 + n // 8, n % 8)
+            if n < 8:
+                add_tile_2(n)
+            if n % 2 == 0:
+                cc = n // 2
+                correct(0, cc, sbs[cc])
+                correct(1, cc, sbs[cc])
+            if n in (6, 8, 10, 12):
+                cc = 4 + (n - 6) // 2
+                sbs[cc] = spread_row_sums(cc)
+        sb2 = {}
+        sb2[0] = spread_row_sums(0)
+        scaled_mean1(2)
+        scaled_mean1(3)
+        row_sums_v1(0, True)
+        row_sums_v1(1, True)
+        for cc in range(1, 4):
+            sb2[cc] = spread_row_sums(cc)
+        kb = pz.tile([P, CW], F32, name="kb", tag="z")
+        for t in range(4):
+            nc.tensor.transpose(kb[:, t * P : (t + 1) * P], cm1[:, t : t + 1].to_broadcast([P, P]), ident[:])
+        nc.scalar.activation(out=ja[:], in_=kb[:], func=FN.Copy, accum_out=k1[:, 0:1])
+
+        hg = {}
+
+        def regroup(c):
+            g_t = work.tile([P, 4 * CW], BF16, name="hg", tag="hg", bufs=2, align_bytes=64)
+            hg[c] = g_t
+            nc.vector.tensor_copy(
+                out=g_t[:].rearrange("p (c i t) -> p c t i", i=4, t=4),
+                in_=ht[c][:].rearrange("p (t c i) -> p c t i", t=4, i=4),
+            )
+
+        hqs = {}
+
+        def quantise_h(c):
+            hq = work.tile([P, CW], U32, name="hq", tag="hq", bufs=2, align_bytes=64)
+            hs = work.tile([P, CW], U8, name="hs", tag="hs", bufs=2, align_bytes=64)
+            nc.vector.quantize_mx(out=hq[:].bitcast(FP8X4), scales=hs[:], in_=hg[c][:])
+            v2[c] = keep.tile([P, 4 * CW], F32, name="v2_%d" % c, tag="hv%d" % c)
+            hqs[c] = (hq, hs)
+
+        def layer2(c, tiles):
+            hq, hs = hqs[c]
+            for t in tiles:
+                z = pz.tile([P, CW], F32, name="z2", tag="z")
+                nc.tensor.matmul_mx(
+                    out=z[:],
+                    lhsT=w2q[:, t * P : (t + 1) * P].bitcast(FP8X4),
+                    lhsT_scale=w2s[:, t * P : (t + 1) * P],
+                    rhs=hq[:].bitcast(FP8X4),
+                    rhs_scale=hs[:],
+                    start=True,
+                    stop=True,
+                )
+                nc.scalar.activation(
+                    out=v2[c][:, t * CW : (t + 1) * CW],
+                    in_=z[:],
+                    func=FN.Relu,
+                    bias=b2f[:, t : t + 1],
+                    scale=1.0,
+                    accum_out=acc2[:, t * CH + c : t * CH + c + 1],
+                )
+
+        svbank = None
+        for c in range(CH):
+            if 1 <= c <= 6:
+                svbank = row_sums_v1(c + 1, False)
+            correct(2, c, sb2[c])
+            correct(3, c, sb2[c])
+            if c >= 1:
+                quantise_h(c - 1)
+            if 1 <= c <= 6:
+                reduce_row_sums(c + 1, svbank)
+            if c >= 1:
+                layer2(c - 1, (0, 1, 2, 3))
+            if c + 4 < CH:
+                sb2[c + 4] = spread_row_sums(c + 4)
+            regroup(c)
+            if c == 0:
+                nc.vector.tensor_reduce(
+                    out=s1[:], in_=acc1[:].rearrange("p (t c) -> p t c", t=4), axis=AXIS.X, op=ALU.add
+                )
+                m1b = pz.tile([P, CW], F32, name="m1b", tag="z")
+                for t in range(4):
+                    nc.tensor.transpose(m1b[:, t * P : (t + 1) * P], s1[:, t : t + 1].to_broadcast([P, P]), ident[:])
+                nc.scalar.activation(
+                    out=m1r[0:32, :].rearrange("p (k t) -> p k t", t=4),
+                    in_=m1b[0:32, :].rearrange("p (t k) -> p k t", t=4),
+                    func=FN.Copy,
+                    scale=1.0 / ROWS,
+                )
+                nc.sync.dma_start(out=out_1.rearrange("(o n) -> o n", o=1), in_=m1r[0:1, :])
+        quantise_h(CH - 1)
+        layer2(CH - 1, (0, 1, 2, 3))
+
+        sh_v = sh[:].rearrange("p (c l) -> p c l", l=4)
+        sx_v = sx[:].rearrange("p (c l) -> p c l", l=4)
+        sv_v = sv[:].rearrange("p (c l) -> p c l", l=4)
+        nc.vector.scalar_tensor_tensor(
+            out=sh_v[:, :, 0:3], in0=sx_v[:, :, 0:3], scalar=k1[:, 0:1], in1=sv_v[:, :, 0:3], op0=ALU.mult, op1=ALU.add
+        )
+        nc.vector.scalar_tensor_tensor(
+            out=sh_v[:, :, 3], in0=sxa[:], scalar=k1[:, 0:1], in1=sv_v[:, :, 3], op0=ALU.mult, op1=ALU.add
+        )
+
+        def natural(a):
+            bank = pt.tile([P, CW], F32, name="vn", tag="pt")
+            for t in range(4):
+                first = t * CW + (a % 4) * P
+                nc.tensor.transpose(bank[:, t * P : (t + 1) * P], v2[a // 4][:, first : first + P], ident[:])
+            return bank
+
+        vn = {}
+        for a in range(4):
+            vn[a] = natural(a)
+        nc.vector.tensor_reduce(out=s2[:], in_=acc2[:].rearrange("p (t c) -> p t c", t=4), axis=AXIS.X, op=ALU.add)
+        mb = pz.tile([P, CW], F32, name="mb", tag="z")
+        for t in range(4):
+            nc.tensor.transpose(mb[:, t * P : (t + 1) * P], s2[:, t : t + 1].to_broadcast([P, P]), ident[:])
+        nc.scalar.activation(out=cm2b[:], in_=mb[:], func=FN.Copy, scale=C / ROWS)
+        nc.scalar.activation(out=m2r[0:32, :], in_=mb[0:32, :], func=FN.Copy, scale=1.0 / ROWS)
+        nc.sync.dma_start(out=out_2.rearrange("(o n) -> o n", o=1), in_=m2r[0:1, :])
+
+        ob = None
+        for a in range(NT):
+            if a % 2 == 0:
+                ob = work.tile([P, 2 * D2], F32, name="ob", tag="ob", bufs=4)
+            nc.vector.scalar_tensor_tensor(
+                out=ob[:, (a % 2) * D2 : (a % 2 + 1) * D2],
+                in0=cm2b[:],
+                scalar=sh[:, a : a + 1],
+                in1=vn[a][:],
+                op0=ALU.mult,
+                op1=ALU.add,
+            )
+            if a % 2 == 1:
+                nc.sync.dma_start(out=out_v[:, (a - 1) * D2 : (a + 1) * D2], in_=ob[:])
+            if a + 4 < NT:
+                vn[a + 4] = natural(a + 4)

@@ -35,7 +35,6 @@ def tile_optimalnet_pa_t_kernel(tc, x, W1, b1, W2, b2, out_0, out_1, out_2):
         ht = {}
         hv = [keep.tile([P, 4 * CW], F32, name="hv%d" % c) for c in range(CH)]
         xq = [keep.tile([P, 2 * CW], U32, name="xq%d" % c, align_bytes=64) for c in range(CH)]
-        sacc = [keep.tile([P, CW], F32, name="sacc%d" % c) for c in range(CH)]
         xs = [keep.tile([P, 2 * CW], U8, name="xs%d" % c, align_bytes=64) for c in range(CH)]
         w1q = keep.tile([P, 1024], U32, name="w1q", align_bytes=64)
         w1s = keep.tile([P, 1024], U8, name="w1s", align_bytes=64)
@@ -100,12 +99,6 @@ def tile_optimalnet_pa_t_kernel(tc, x, W1, b1, W2, b2, out_0, out_1, out_2):
                 accum_out=acc1[:, t * CH + c : t * CH + c + 1],
             )
 
-        def add_tiles_01(c):
-            nc.gpsimd.tensor_tensor(out=sacc[c][:], in0=hv[c][:, 0:CW], in1=hv[c][:, CW : 2 * CW], op=ALU.add)
-
-        def add_tile_2(c):
-            nc.gpsimd.tensor_tensor(out=sacc[c][:], in0=sacc[c][:], in1=hv[c][:, 2 * CW : 3 * CW], op=ALU.add)
-
         def spread_row_sums(c):
             sb = pt.tile([P, CW], F32, name="sb", tag="pt")
             for l in range(4):
@@ -134,15 +127,14 @@ def tile_optimalnet_pa_t_kernel(tc, x, W1, b1, W2, b2, out_0, out_1, out_2):
         def row_sums_v1(c, on_scalar):
             bank = pz.tile([P, CW], F32, name="svb", tag="z")
             for l in range(4):
-                parts = (sacc[c][:, l * P : (l + 1) * P], hv[c][:, 3 * CW + l * P : 3 * CW + (l + 1) * P])
-                for k in range(2):
+                for t in range(4):
                     nc.tensor.matmul(
                         out=bank[:, l * P : (l + 1) * P],
-                        lhsT=parts[k],
+                        lhsT=hv[c][:, t * CW + l * P : t * CW + (l + 1) * P],
                         rhs=ident[:],
                         is_transpose=True,
-                        start=(k == 0),
-                        stop=(k == 1),
+                        start=(t == 0),
+                        stop=(t == 3),
                     )
             if on_scalar:
                 for l in range(4):
@@ -248,7 +240,6 @@ def tile_optimalnet_pa_t_kernel(tc, x, W1, b1, W2, b2, out_0, out_1, out_2):
                     for cc in range(4):
                         sbs[cc] = spread_row_sums(cc)
                 layer1(1, c)
-                add_tiles_01(c)
                 if c == 0:
                     load_x(7)
                 if c == 2:
@@ -281,8 +272,6 @@ def tile_optimalnet_pa_t_kernel(tc, x, W1, b1, W2, b2, out_0, out_1, out_2):
         scaled_mean1(1)
         for n in range(16):
             layer1(2 + n // 8, n % 8)
-            if n < 8:
-                add_tile_2(n)
             if n % 2 == 0:
                 cc = n // 2
                 correct(0, cc, sbs[cc])

@@ -46,8 +46,6 @@ def tile_optimalnet_pa_t_kernel(tc, x, W1, b1, W2, b2, out_0, out_1, out_2):
         acc1 = keep.tile([P, 32], F32, name="acc1")
         acc2 = keep.tile([P, 32], F32, name="acc2")
         sx = keep.tile([P, NT], F32, name="sx")
-        sxa = keep.tile([P, CH], F32, name="sxa")
-        jxa = keep.tile([P, D0], BF16, name="jxa")
         sh = keep.tile([P, NT], F32, name="sh")
         sv = keep.tile([P, NT], F32, name="sv")
         k1 = keep.tile([P, 1], F32, name="k1")
@@ -103,8 +101,7 @@ def tile_optimalnet_pa_t_kernel(tc, x, W1, b1, W2, b2, out_0, out_1, out_2):
             sb = pt.tile([P, CW], F32, name="sb", tag="pt")
             for l in range(4):
                 a = 4 * c + l
-                col = sxa[:, c : c + 1] if l == 3 else sx[:, a : a + 1]
-                nc.tensor.transpose(sb[:, l * P : (l + 1) * P], col.to_broadcast([P, P]), ident[:])
+                nc.tensor.transpose(sb[:, l * P : (l + 1) * P], sx[:, a : a + 1].to_broadcast([P, P]), ident[:])
             return sb
 
         def scaled_mean1(t):
@@ -169,10 +166,7 @@ def tile_optimalnet_pa_t_kernel(tc, x, W1, b1, W2, b2, out_0, out_1, out_2):
                     exit_words(g_t, l * P, bank)
 
             def row_sums_x(c):
-                nc.scalar.activation(
-                    out=jxa[:], in_=xn[c][:, 3 * D0 : 4 * D0], func=FN.Copy, accum_out=sxa[:, c : c + 1]
-                )
-                for l in range(3):
+                for l in range(4):
                     a = 4 * c + l
                     nc.vector.tensor_scalar(
                         out=jx[:],
@@ -365,15 +359,7 @@ def tile_optimalnet_pa_t_kernel(tc, x, W1, b1, W2, b2, out_0, out_1, out_2):
         quantise_h(CH - 1)
         layer2(CH - 1, (0, 1, 2, 3))
 
-        sh_v = sh[:].rearrange("p (c l) -> p c l", l=4)
-        sx_v = sx[:].rearrange("p (c l) -> p c l", l=4)
-        sv_v = sv[:].rearrange("p (c l) -> p c l", l=4)
-        nc.vector.scalar_tensor_tensor(
-            out=sh_v[:, :, 0:3], in0=sx_v[:, :, 0:3], scalar=k1[:, 0:1], in1=sv_v[:, :, 0:3], op0=ALU.mult, op1=ALU.add
-        )
-        nc.vector.scalar_tensor_tensor(
-            out=sh_v[:, :, 3], in0=sxa[:], scalar=k1[:, 0:1], in1=sv_v[:, :, 3], op0=ALU.mult, op1=ALU.add
-        )
+        nc.vector.scalar_tensor_tensor(out=sh[:], in0=sx[:], scalar=k1[:, 0:1], in1=sv[:], op0=ALU.mult, op1=ALU.add)
 
         def natural(a):
             bank = pt.tile([P, CW], F32, name="vn", tag="pt")

@@ -18,13 +18,14 @@ C = 0.01 * 0.001 / 1
 NT = ROWS // P
 CH = 8
 CW = 512
+HALF = D2 // 2
 FLOPS = 2 * ROWS * D0 * D1 + 2 * ROWS * D1 * D2
 
 
 def tile_optimalnet_pa_t_kernel(tc, x, W1, b1, W2, b2, out_0, out_1, out_2):
     nc = tc.nc
     x_v = x.rearrange("(p a) i -> p (a i)", a=NT)
-    out_v = out_0.rearrange("(p a) o -> p (a o)", a=NT)
+    out_v = out_0.rearrange("(p a) o -> p a o", a=NT)
 
     with ExitStack() as ctx:
         ctx.enter_context(tc.manual_schedule())
@@ -32,7 +33,6 @@ def tile_optimalnet_pa_t_kernel(tc, x, W1, b1, W2, b2, out_0, out_1, out_2):
         pt = ctx.enter_context(tc.psum_pool(name="pt", bufs=4))
         pz = ctx.enter_context(tc.psum_pool(name="pz", bufs=4))
 
-        ht = {}
         hv = [keep.tile([P, 4 * CW], F32, name="hv%d" % c) for c in range(CH)]
         xq = [keep.tile([P, 2 * CW], U32, name="xq%d" % c, align_bytes=64) for c in range(CH)]
         xs = [keep.tile([P, 2 * CW], U8, name="xs%d" % c, align_bytes=64) for c in range(CH)]
@@ -59,22 +59,19 @@ def tile_optimalnet_pa_t_kernel(tc, x, W1, b1, W2, b2, out_0, out_1, out_2):
         m2r = keep.tile([P, D2], F32, name="m2r")
         m1r = keep.tile([P, D1], F32, name="m1r")
 
+        zeros = keep.tile([P, CW], F32, name="zeros")
+
         make_identity(nc, ident[:])
+        nc.gpsimd.memset(zeros[:], 0.0)
 
-        def four_transposes(bank, words, first):
-            for b in range(4):
-                g, u = b // 2, b % 2
-                w0 = first + g * 2 * P + u
-                nc.tensor.transpose(bank[:, b * P : (b + 1) * P], words[:, w0 : first + (g + 1) * 2 * P : 2], ident[:])
+        def spread_row_sums(c):
+            sb = pt.tile([P, CW], F32, name="sb", tag="pt")
+            for l in range(4):
+                a = 4 * c + l
+                nc.tensor.transpose(sb[:, l * P : (l + 1) * P], sx[:, a : a + 1].to_broadcast([P, P]), ident[:])
+            return sb
 
-        def exit_words(grouped, col0, bank):
-            dst = grouped[:].bitcast(F32).rearrange("q (g c u) -> q g c u", g=2, u=2)
-            nc.scalar.copy(
-                out=dst[:, :, col0 : col0 + P, :],
-                in_=bank[:].rearrange("q (g u c) -> q g c u", g=2, u=2),
-            )
-
-        def layer1(t, c):
+        def layer1(t, c, on_vector=False):
             z = pz.tile([P, CW], F32, name="z", tag="z")
             for g in range(2):
                 wcols = slice(g * 512 + t * P, g * 512 + (t + 1) * P)
@@ -88,21 +85,22 @@ def tile_optimalnet_pa_t_kernel(tc, x, W1, b1, W2, b2, out_0, out_1, out_2):
                     start=(g == 0),
                     stop=(g == 1),
                 )
-            nc.scalar.activation(
-                out=hv[c][:, t * CW : (t + 1) * CW],
-                in_=z[:],
-                func=FN.Relu,
-                bias=b1f[:, t : t + 1],
-                scale=1.0,
-                accum_out=acc1[:, t * CH + c : t * CH + c + 1],
-            )
-
-        def spread_row_sums(c):
-            sb = pt.tile([P, CW], F32, name="sb", tag="pt")
-            for l in range(4):
-                a = 4 * c + l
-                nc.tensor.transpose(sb[:, l * P : (l + 1) * P], sx[:, a : a + 1].to_broadcast([P, P]), ident[:])
-            return sb
+            v1 = hv[c][:, t * CW : (t + 1) * CW]
+            total = acc1[:, t * CH + c : t * CH + c + 1]
+            if on_vector:
+                nc.vector.scalar_tensor_tensor(
+                    out=v1,
+                    in0=z[:],
+                    scalar=b1f[:, t : t + 1],
+                    in1=zeros[:],
+                    op0=ALU.add,
+                    op1=ALU.max,
+                    accum_out=total,
+                )
+            else:
+                nc.scalar.activation(
+                    out=v1, in_=z[:], func=FN.Relu, bias=b1f[:, t : t + 1], scale=1.0, accum_out=total
+                )
 
         def scaled_mean1(t):
             nc.vector.tensor_scalar(
@@ -115,55 +113,40 @@ def tile_optimalnet_pa_t_kernel(tc, x, W1, b1, W2, b2, out_0, out_1, out_2):
                 accum_out=cm1[:, t : t + 1],
             )
 
-        def correct(t, c, sb):
-            seg = slice(t * CW, (t + 1) * CW)
-            nc.vector.scalar_tensor_tensor(
-                out=ht[c][:, seg], in0=sb[:], scalar=cm1[:, t : t + 1], in1=hv[c][:, seg], op0=ALU.mult, op1=ALU.add
-            )
-
-        def row_sums_v1(c, on_scalar):
-            bank = pz.tile([P, CW], F32, name="svb", tag="z")
-            for l in range(4):
-                for t in range(4):
-                    nc.tensor.matmul(
-                        out=bank[:, l * P : (l + 1) * P],
-                        lhsT=hv[c][:, t * CW + l * P : t * CW + (l + 1) * P],
-                        rhs=ident[:],
-                        is_transpose=True,
-                        start=(t == 0),
-                        stop=(t == 3),
-                    )
-            if on_scalar:
-                for l in range(4):
-                    a = 4 * c + l
-                    nc.scalar.activation(
-                        out=ja[:, 0:P], in_=bank[:, l * P : (l + 1) * P], func=FN.Copy, accum_out=sv[:, a : a + 1]
-                    )
-            return bank
-
-        def reduce_row_sums(c, bank):
-            nc.vector.tensor_reduce(
-                out=sv[:, 4 * c : 4 * c + 4], in_=bank[:].rearrange("p (l k) -> p l k", l=4), axis=AXIS.X, op=ALU.add
-            )
-
+        sbs = {}
         with tc.tile_pool(name="stage", bufs=1) as stage:
             xn = {}
-
-            def load_x(c):
-                xt = stage.tile([P, 4 * D0], BF16, name="xn", tag="xn", bufs=5)
-                nc.sync.dma_start(out=xt[:], in_=x_v[:, c * 4 * D0 : (c + 1) * 4 * D0])
-                xn[c] = xt
-
             xg = {}
 
+            def load_x(c, pieces):
+                xt = stage.tile([P, 4 * D0], BF16, name="xn", tag="xn", bufs=5)
+                n = 4 * D0 // pieces
+                for i in range(pieces):
+                    nc.sync.dma_start(
+                        out=xt[:, i * n : (i + 1) * n], in_=x_v[:, c * 4 * D0 + i * n : c * 4 * D0 + (i + 1) * n]
+                    )
+                xn[c] = xt
+
+            def words_to_k(words, first, grouped, col0, on_vector):
+                bank = pt.tile([P, CW], F32, name="xt", tag="pt")
+                for g in range(2):
+                    for u in range(2):
+                        b = 2 * g + u
+                        w0 = first + g * 2 * P + u
+                        nc.tensor.transpose(
+                            bank[:, b * P : (b + 1) * P], words[:, w0 : first + (g + 1) * 2 * P : 2], ident[:]
+                        )
+                dst = grouped[:].bitcast(F32).rearrange("q (g c u) -> q g c u", g=2, u=2)[:, :, col0 : col0 + P, :]
+                src = bank[:].rearrange("q (g u c) -> q g c u", g=2, u=2)
+                if on_vector:
+                    nc.vector.tensor_copy(out=dst, in_=src)
+                else:
+                    nc.scalar.copy(out=dst, in_=src)
+
             def transpose_x(c):
-                g_t = stage.tile([P, 4 * D0], BF16, name="xg", tag="xg", bufs=2, align_bytes=64)
-                xg[c] = g_t
-                words = xn[c][:].bitcast(F32)
+                xg[c] = stage.tile([P, 4 * D0], BF16, name="xg", tag="xg", bufs=2, align_bytes=64)
                 for l in range(4):
-                    bank = pt.tile([P, CW], F32, name="xt", tag="pt")
-                    four_transposes(bank, words, l * 512)
-                    exit_words(g_t, l * P, bank)
+                    words_to_k(xn[c][:].bitcast(F32), l * 512, xg[c], l * P, False)
 
             def row_sums_x(c):
                 for l in range(4):
@@ -189,17 +172,13 @@ def tile_optimalnet_pa_t_kernel(tc, x, W1, b1, W2, b2, out_0, out_1, out_2):
             b2r = stage.tile([4, P], BF16, name="b2r")
             b2pad = stage.tile([P, P], F32, name="b2pad")
 
-            first = stage.tile([P, 4 * D0], BF16, name="xn", tag="xn", bufs=5)
-            xn[0] = first
-            for l in range(4):
-                nc.sync.dma_start(out=first[:, l * D0 : (l + 1) * D0], in_=x_v[:, l * D0 : (l + 1) * D0])
+            load_x(0, 4)
             nc.sync.dma_start(out=w1n[:], in_=W1.rearrange("(p t) i -> p (t i)", t=4))
-            load_x(1)
+            for c in range(1, 5):
+                load_x(c, 1)
             nc.sync.dma_start(
                 out=w2n[:].rearrange("p (t o) -> p t o", t=4), in_=W2.rearrange("(t p) o -> p t o", p=P)
             )
-            for c in range(2, 5):
-                load_x(c)
             nc.scalar.dma_start(out=b1r[:], in_=b1.rearrange("(p t) -> p t", t=4))
             nc.scalar.dma_start(out=b2r[:], in_=b2.rearrange("(t p) -> t p", p=P))
 
@@ -209,34 +188,25 @@ def tile_optimalnet_pa_t_kernel(tc, x, W1, b1, W2, b2, out_0, out_1, out_2):
 
             transpose_x(0)
             row_sums_x(0)
-            w1words = w1n[:].bitcast(F32)
+            quantise_x(0)
             for t in range(4):
-                bank = pt.tile([P, CW], F32, name="w1t", tag="pt")
-                four_transposes(bank, w1words, t * 512)
-                exit_words(w1g, t * P, bank)
-            nc.vector.quantize_mx(out=w1q[:].bitcast(FP8X4), scales=w1s[:], in_=w1g[:])
+                words_to_k(w1n[:].bitcast(F32), t * 512, w1g, t * P, t % 2 == 1)
             transpose_x(1)
+            nc.vector.quantize_mx(out=w1q[:].bitcast(FP8X4), scales=w1s[:], in_=w1g[:])
             row_sums_x(1)
-            load_x(5)
-            load_x(6)
 
-            sbs = {}
             for c in range(CH):
-                quantise_x(c)
-                if c + 2 < CH - 2:
-                    row_sums_x(c + 2)
-                if c >= CH - 2:
-                    row_sums_x(c)
+                if c + 5 < CH:
+                    load_x(c + 5, 1)
                 layer1(0, c)
+                layer1(1, c, c >= CH - 2)
+                layer1(2, c)
+                if c + 1 < CH:
+                    quantise_x(c + 1)
                 if c + 2 < CH:
                     transpose_x(c + 2)
-                if c == CH - 1:
-                    for cc in range(4):
-                        sbs[cc] = spread_row_sums(cc)
-                layer1(1, c)
-                if c == 0:
-                    load_x(7)
-                if c == 2:
+                    row_sums_x(c + 2)
+                if c == CH - 2:
                     w2words = w2n[:].bitcast(F32).rearrange("p (t w u) -> p t u w", t=4, u=2)
                     w2gw = w2g[:].bitcast(F32).rearrange("q (t c u) -> q t c u", t=4, u=2)
                     for h in range(2):
@@ -247,151 +217,191 @@ def tile_optimalnet_pa_t_kernel(tc, x, W1, b1, W2, b2, out_0, out_1, out_2):
                                 nc.tensor.transpose(
                                     bank[:, k * P : (k + 1) * P], w2words[:, 2 * h + tl, u, :], ident[:]
                                 )
-                        nc.scalar.copy(
+                        nc.vector.tensor_copy(
                             out=w2gw[:, 2 * h : 2 * h + 2, :, :],
                             in_=bank[:].rearrange("q (t u c) -> q t c u", t=2, u=2),
                         )
                     bank = pt.tile([P, CW], F32, name="b2t", tag="pt")
                     nc.tensor.transpose(bank[:, 0:P], b2pad[:], ident[:])
-                    nc.scalar.copy(out=b2f[:], in_=bank[:, 0:4])
-                if c == 3:
+                    nc.vector.tensor_copy(out=b2f[:], in_=bank[:, 0:4])
                     nc.vector.quantize_mx(out=w2q[:].bitcast(FP8X4), scales=w2s[:], in_=w2g[:])
+                    sbs[0] = spread_row_sums(0)
+            for c in range(1, 4):
+                sbs[c] = spread_row_sums(c)
 
         work = ctx.enter_context(tc.tile_pool(name="work", bufs=1))
-        for c in range(CH):
-            ht[c] = work.tile([P, 4 * CW], BF16, name="ht%d" % c)
+        hq = [work.tile([P, CW], U32, name="hq%d" % c, align_bytes=64) for c in range(CH)]
+        hs = [work.tile([P, CW], U8, name="hs%d" % c, align_bytes=64) for c in range(CH)]
+        ht = {}
+        hg = {}
         v2 = {}
 
-        scaled_mean1(0)
-        scaled_mean1(1)
-        for n in range(16):
-            layer1(2 + n // 8, n % 8)
-            if n % 2 == 0:
-                cc = n // 2
-                correct(0, cc, sbs[cc])
-                correct(1, cc, sbs[cc])
-            if n in (6, 8, 10, 12):
-                cc = 4 + (n - 6) // 2
-                sbs[cc] = spread_row_sums(cc)
-        sb2 = {}
-        sb2[0] = spread_row_sums(0)
-        scaled_mean1(2)
-        scaled_mean1(3)
-        row_sums_v1(0, True)
-        row_sums_v1(1, True)
-        for cc in range(1, 4):
-            sb2[cc] = spread_row_sums(cc)
-        kb = pz.tile([P, CW], F32, name="kb", tag="z")
-        for t in range(4):
-            nc.tensor.transpose(kb[:, t * P : (t + 1) * P], cm1[:, t : t + 1].to_broadcast([P, P]), ident[:])
-        nc.scalar.activation(out=ja[:], in_=kb[:], func=FN.Copy, accum_out=k1[:, 0:1])
-
-        hg = {}
-
-        def regroup(c):
-            g_t = work.tile([P, 4 * CW], BF16, name="hg", tag="hg", bufs=2, align_bytes=64)
-            hg[c] = g_t
-            nc.vector.tensor_copy(
-                out=g_t[:].rearrange("p (c i t) -> p c t i", i=4, t=4),
-                in_=ht[c][:].rearrange("p (t c i) -> p c t i", t=4, i=4),
-            )
-
-        hqs = {}
-
-        def quantise_h(c):
-            hq = work.tile([P, CW], U32, name="hq", tag="hq", bufs=2, align_bytes=64)
-            hs = work.tile([P, CW], U8, name="hs", tag="hs", bufs=2, align_bytes=64)
-            nc.vector.quantize_mx(out=hq[:].bitcast(FP8X4), scales=hs[:], in_=hg[c][:])
-            v2[c] = keep.tile([P, 4 * CW], F32, name="v2_%d" % c, tag="hv%d" % c)
-            hqs[c] = (hq, hs)
-
-        def layer2(c, tiles):
-            hq, hs = hqs[c]
-            for t in tiles:
-                z = pz.tile([P, CW], F32, name="z2", tag="z")
-                nc.tensor.matmul_mx(
-                    out=z[:],
-                    lhsT=w2q[:, t * P : (t + 1) * P].bitcast(FP8X4),
-                    lhsT_scale=w2s[:, t * P : (t + 1) * P],
-                    rhs=hq[:].bitcast(FP8X4),
-                    rhs_scale=hs[:],
-                    start=True,
-                    stop=True,
-                )
-                nc.scalar.activation(
-                    out=v2[c][:, t * CW : (t + 1) * CW],
-                    in_=z[:],
-                    func=FN.Relu,
-                    bias=b2f[:, t : t + 1],
-                    scale=1.0,
-                    accum_out=acc2[:, t * CH + c : t * CH + c + 1],
-                )
-
-        svbank = None
-        for c in range(CH):
-            if 1 <= c <= 6:
-                svbank = row_sums_v1(c + 1, False)
-            correct(2, c, sb2[c])
-            correct(3, c, sb2[c])
-            if c >= 1:
-                quantise_h(c - 1)
-            if 1 <= c <= 6:
-                reduce_row_sums(c + 1, svbank)
-            if c >= 1:
-                layer2(c - 1, (0, 1, 2, 3))
-            if c + 4 < CH:
-                sb2[c + 4] = spread_row_sums(c + 4)
-            regroup(c)
-            if c == 0:
-                nc.vector.tensor_reduce(
-                    out=s1[:], in_=acc1[:].rearrange("p (t c) -> p t c", t=4), axis=AXIS.X, op=ALU.add
-                )
-                m1b = pz.tile([P, CW], F32, name="m1b", tag="z")
-                for t in range(4):
-                    nc.tensor.transpose(m1b[:, t * P : (t + 1) * P], s1[:, t : t + 1].to_broadcast([P, P]), ident[:])
-                nc.scalar.activation(
-                    out=m1r[0:32, :].rearrange("p (k t) -> p k t", t=4),
-                    in_=m1b[0:32, :].rearrange("p (t k) -> p k t", t=4),
-                    func=FN.Copy,
-                    scale=1.0 / ROWS,
-                )
-                nc.sync.dma_start(out=out_1.rearrange("(o n) -> o n", o=1), in_=m1r[0:1, :])
-        quantise_h(CH - 1)
-        layer2(CH - 1, (0, 1, 2, 3))
-
-        nc.vector.scalar_tensor_tensor(out=sh[:], in0=sx[:], scalar=k1[:, 0:1], in1=sv[:], op0=ALU.mult, op1=ALU.add)
-
-        def natural(a):
-            bank = pt.tile([P, CW], F32, name="vn", tag="pt")
-            for t in range(4):
-                first = t * CW + (a % 4) * P
-                nc.tensor.transpose(bank[:, t * P : (t + 1) * P], v2[a // 4][:, first : first + P], ident[:])
-            return bank
-
-        vn = {}
-        for a in range(4):
-            vn[a] = natural(a)
-        nc.vector.tensor_reduce(out=s2[:], in_=acc2[:].rearrange("p (t c) -> p t c", t=4), axis=AXIS.X, op=ALU.add)
-        mb = pz.tile([P, CW], F32, name="mb", tag="z")
-        for t in range(4):
-            nc.tensor.transpose(mb[:, t * P : (t + 1) * P], s2[:, t : t + 1].to_broadcast([P, P]), ident[:])
-        nc.scalar.activation(out=cm2b[:], in_=mb[:], func=FN.Copy, scale=C / ROWS)
-        nc.scalar.activation(out=m2r[0:32, :], in_=mb[0:32, :], func=FN.Copy, scale=1.0 / ROWS)
-        nc.sync.dma_start(out=out_2.rearrange("(o n) -> o n", o=1), in_=m2r[0:1, :])
-
-        ob = None
-        for a in range(NT):
-            if a % 2 == 0:
-                ob = work.tile([P, 2 * D2], F32, name="ob", tag="ob", bufs=4)
+        def correct(t, c):
+            if t == 0:
+                ht[c] = work.tile([P, 4 * CW], BF16, name="ht", tag="ht", bufs=6)
+            seg = slice(t * CW, (t + 1) * CW)
             nc.vector.scalar_tensor_tensor(
-                out=ob[:, (a % 2) * D2 : (a % 2 + 1) * D2],
-                in0=cm2b[:],
-                scalar=sh[:, a : a + 1],
-                in1=vn[a][:],
+                out=ht[c][:, seg],
+                in0=sbs[c][:],
+                scalar=cm1[:, t : t + 1],
+                in1=hv[c][:, seg],
                 op0=ALU.mult,
                 op1=ALU.add,
             )
-            if a % 2 == 1:
-                nc.sync.dma_start(out=out_v[:, (a - 1) * D2 : (a + 1) * D2], in_=ob[:])
-            if a + 4 < NT:
-                vn[a + 4] = natural(a + 4)
+
+        def row_sums_v1(c):
+            bank = pz.tile([P, CW], F32, name="svb", tag="z")
+            for l in range(4):
+                for t in range(4):
+                    nc.tensor.matmul(
+                        out=bank[:, l * P : (l + 1) * P],
+                        lhsT=hv[c][:, t * CW + l * P : t * CW + (l + 1) * P],
+                        rhs=ident[:],
+                        is_transpose=True,
+                        start=(t == 0),
+                        stop=(t == 3),
+                    )
+            for l in range(4):
+                a = 4 * c + l
+                nc.scalar.activation(
+                    out=ja[:, 0:P], in_=bank[:, l * P : (l + 1) * P], func=FN.Copy, accum_out=sv[:, a : a + 1]
+                )
+
+        def regroup(c):
+            hg[c] = work.tile([P, 4 * CW], BF16, name="hg", tag="hg", bufs=3, align_bytes=64)
+            dst = hg[c][:].rearrange("p (c i t) -> p c t i", i=4, t=4)
+            src = ht[c][:].rearrange("p (t c i) -> p c t i", t=4, i=4)
+            if c in (2, 4, 6):
+                nc.scalar.copy(out=dst, in_=src)
+            else:
+                nc.vector.tensor_copy(out=dst, in_=src)
+
+        def quantise_h(c):
+            nc.vector.quantize_mx(out=hq[c][:].bitcast(FP8X4), scales=hs[c][:], in_=hg[c][:])
+
+        def layer2(t, c):
+            if t == 0:
+                v2[c] = keep.tile([P, 4 * CW], F32, name="v2_%d" % c, tag="hv%d" % c)
+            z = pz.tile([P, CW], F32, name="z2", tag="z")
+            nc.tensor.matmul_mx(
+                out=z[:],
+                lhsT=w2q[:, t * P : (t + 1) * P].bitcast(FP8X4),
+                lhsT_scale=w2s[:, t * P : (t + 1) * P],
+                rhs=hq[c][:].bitcast(FP8X4),
+                rhs_scale=hs[c][:],
+                start=True,
+                stop=True,
+            )
+            nc.scalar.activation(
+                out=v2[c][:, t * CW : (t + 1) * CW],
+                in_=z[:],
+                func=FN.Relu,
+                bias=b2f[:, t : t + 1],
+                scale=1.0,
+                accum_out=acc2[:, t * CH + c : t * CH + c + 1],
+            )
+
+        def sum_of_means():
+            kb = pz.tile([P, CW], F32, name="kb", tag="z")
+            for t in range(4):
+                nc.tensor.transpose(kb[:, t * P : (t + 1) * P], cm1[:, t : t + 1].to_broadcast([P, P]), ident[:])
+            nc.scalar.activation(out=ja[:], in_=kb[:], func=FN.Copy, accum_out=k1[:, 0:1])
+
+        def store_m1():
+            nc.vector.tensor_reduce(
+                out=s1[:], in_=acc1[:].rearrange("p (t c) -> p t c", t=4), axis=AXIS.X, op=ALU.add
+            )
+            m1b = pz.tile([P, CW], F32, name="m1b", tag="z")
+            for t in range(4):
+                nc.tensor.transpose(m1b[:, t * P : (t + 1) * P], s1[:, t : t + 1].to_broadcast([P, P]), ident[:])
+            nc.scalar.activation(
+                out=m1r[0:32, :].rearrange("p (k t) -> p k t", t=4),
+                in_=m1b[0:32, :].rearrange("p (t k) -> p k t", t=4),
+                func=FN.Copy,
+                scale=1.0 / ROWS,
+            )
+            nc.sync.dma_start(out=out_1.rearrange("(o n) -> o n", o=1), in_=m1r[0:1, :])
+
+        LEAD = 3
+        for t in range(3):
+            scaled_mean1(t)
+        for c in range(CH):
+            layer1(3, c)
+        for c in range(LEAD):
+            for t in range(3):
+                correct(t, c)
+        scaled_mean1(3)
+        for c in range(CH):
+            for t in range(3 if c < LEAD else 0, 4):
+                correct(t, c)
+            row_sums_v1(c)
+            if c + 4 < CH:
+                sbs[c + 4] = spread_row_sums(c + 4)
+            if c >= 2:
+                quantise_h(c - 2)
+                layer2(0, c - 2)
+                layer2(1, c - 2)
+            regroup(c)
+            if c == 0:
+                sum_of_means()
+            if c == 1:
+                store_m1()
+        for c in range(CH - 2, CH):
+            quantise_h(c)
+            layer2(0, c)
+            layer2(1, c)
+
+        def natural(h, j):
+            bank = pt.tile([P, CW], F32, name="vn", tag="pt")
+            for k in range(2):
+                a = 2 * j + k
+                for tl in range(2):
+                    first = (2 * h + tl) * CW + (a % 4) * P
+                    col = (2 * k + tl) * P
+                    nc.tensor.transpose(bank[:, col : col + P], v2[a // 4][:, first : first + P], ident[:])
+            return bank
+
+        def means2(h):
+            cols = slice(h * HALF, (h + 1) * HALF)
+            nc.vector.tensor_reduce(
+                out=s2[:, 2 * h : 2 * h + 2],
+                in_=acc2[:, 16 * h : 16 * h + 16].rearrange("p (t c) -> p t c", t=2),
+                axis=AXIS.X,
+                op=ALU.add,
+            )
+            mb = pz.tile([P, CW], F32, name="mb", tag="z")
+            for tl in range(2):
+                t = 2 * h + tl
+                nc.tensor.transpose(mb[:, tl * P : (tl + 1) * P], s2[:, t : t + 1].to_broadcast([P, P]), ident[:])
+            nc.scalar.activation(out=cm2b[:, cols], in_=mb[:, 0:HALF], func=FN.Copy, scale=C / ROWS)
+            nc.scalar.activation(out=m2r[0:32, cols], in_=mb[0:32, 0:HALF], func=FN.Copy, scale=1.0 / ROWS)
+
+        nc.vector.scalar_tensor_tensor(out=sh[:], in0=sx[:], scalar=k1[:, 0:1], in1=sv[:], op0=ALU.mult, op1=ALU.add)
+
+        for h in range(2):
+            cols = slice(h * HALF, (h + 1) * HALF)
+            means2(h)
+            if h == 1:
+                nc.sync.dma_start(out=out_2.rearrange("(o n) -> o n", o=1), in_=m2r[0:1, :])
+            vn = {}
+            for j in range(4):
+                vn[j] = natural(h, j)
+            for c in range(CH):
+                if h == 0:
+                    layer2(2, c)
+                    layer2(3, c)
+                ob = work.tile([P, 4, HALF], F32, name="ob", tag="ob", bufs=4)
+                for j in (2 * c, 2 * c + 1):
+                    for k in range(2):
+                        a = 2 * j + k
+                        nc.vector.scalar_tensor_tensor(
+                            out=ob[:, a % 4, :],
+                            in0=cm2b[:, cols],
+                            scalar=sh[:, a : a + 1],
+                            in1=vn[j][:, k * HALF : (k + 1) * HALF],
+                            op0=ALU.mult,
+                            op1=ALU.add,
+                        )
+                    if j + 4 < NT // 2:
+                        vn[j + 4] = natural(h, j + 4)
+                nc.sync.dma_start(out=out_v[:, 4 * c : 4 * c + 4, cols], in_=ob[:])

@@ -71,6 +71,15 @@ def tile_optimalnet_pa_t_kernel(tc, x, W1, b1, W2, b2, out_0, out_1, out_2):
                 nc.tensor.transpose(sb[:, l * P : (l + 1) * P], sx[:, a : a + 1].to_broadcast([P, P]), ident[:])
             return sb
 
+        def relu_and_sum(on_vector, v, z, bias, acc, col):
+            total = acc[:, col : col + 1]
+            if on_vector:
+                nc.vector.scalar_tensor_tensor(
+                    out=v, in0=z[:], scalar=bias, in1=zeros[:], op0=ALU.add, op1=ALU.max, accum_out=total
+                )
+            else:
+                nc.scalar.activation(out=v, in_=z[:], func=FN.Relu, bias=bias, scale=1.0, accum_out=total)
+
         def layer1(t, c, on_vector=False):
             z = pz.tile([P, CW], F32, name="z", tag="z")
             for g in range(2):
@@ -85,22 +94,7 @@ def tile_optimalnet_pa_t_kernel(tc, x, W1, b1, W2, b2, out_0, out_1, out_2):
                     start=(g == 0),
                     stop=(g == 1),
                 )
-            v1 = hv[c][:, t * CW : (t + 1) * CW]
-            total = acc1[:, t * CH + c : t * CH + c + 1]
-            if on_vector:
-                nc.vector.scalar_tensor_tensor(
-                    out=v1,
-                    in0=z[:],
-                    scalar=b1f[:, t : t + 1],
-                    in1=zeros[:],
-                    op0=ALU.add,
-                    op1=ALU.max,
-                    accum_out=total,
-                )
-            else:
-                nc.scalar.activation(
-                    out=v1, in_=z[:], func=FN.Relu, bias=b1f[:, t : t + 1], scale=1.0, accum_out=total
-                )
+            relu_and_sum(on_vector, hv[c][:, t * CW : (t + 1) * CW], z, b1f[:, t : t + 1], acc1, t * CH + c)
 
         def scaled_mean1(t):
             nc.vector.tensor_scalar(
@@ -172,6 +166,8 @@ def tile_optimalnet_pa_t_kernel(tc, x, W1, b1, W2, b2, out_0, out_1, out_2):
             b2r = stage.tile([4, P], BF16, name="b2r")
             b2pad = stage.tile([P, P], F32, name="b2pad")
 
+            nc.sync.dma_start(out=b1r[:], in_=b1.rearrange("(p t) -> p t", t=4))
+            nc.sync.dma_start(out=b2r[:], in_=b2.rearrange("(t p) -> t p", p=P))
             load_x(0, 4)
             nc.sync.dma_start(out=w1n[:], in_=W1.rearrange("(p t) i -> p (t i)", t=4))
             for c in range(1, 5):
@@ -179,34 +175,31 @@ def tile_optimalnet_pa_t_kernel(tc, x, W1, b1, W2, b2, out_0, out_1, out_2):
             nc.sync.dma_start(
                 out=w2n[:].rearrange("p (t o) -> p t o", t=4), in_=W2.rearrange("(t p) o -> p t o", p=P)
             )
-            nc.scalar.dma_start(out=b1r[:], in_=b1.rearrange("(p t) -> p t", t=4))
-            nc.scalar.dma_start(out=b2r[:], in_=b2.rearrange("(t p) -> t p", p=P))
-
-            nc.vector.memset(b2pad[:], 0.0)
-            nc.vector.tensor_copy(out=b1f[:], in_=b1r[:])
-            nc.vector.tensor_copy(out=b2pad[0:4, :], in_=b2r[:])
 
             transpose_x(0)
             row_sums_x(0)
+            nc.vector.tensor_copy(out=b1f[:], in_=b1r[:])
+            nc.vector.memset(b2pad[:], 0.0)
+            nc.vector.tensor_copy(out=b2pad[0:4, :], in_=b2r[:])
             quantise_x(0)
             for t in range(4):
                 words_to_k(w1n[:].bitcast(F32), t * 512, w1g, t * P, t % 2 == 1)
             transpose_x(1)
             nc.vector.quantize_mx(out=w1q[:].bitcast(FP8X4), scales=w1s[:], in_=w1g[:])
-            row_sums_x(1)
 
             for c in range(CH):
                 if c + 5 < CH:
                     load_x(c + 5, 1)
                 layer1(0, c)
-                layer1(1, c, c >= CH - 2)
+                layer1(1, c, c == CH - 1)
                 layer1(2, c)
                 if c + 1 < CH:
                     quantise_x(c + 1)
                 if c + 2 < CH:
                     transpose_x(c + 2)
-                    row_sums_x(c + 2)
-                if c == CH - 2:
+                if c + 1 < CH:
+                    row_sums_x(c + 1)
+                if c == 3:
                     w2words = w2n[:].bitcast(F32).rearrange("p (t w u) -> p t u w", t=4, u=2)
                     w2gw = w2g[:].bitcast(F32).rearrange("q (t c u) -> q t c u", t=4, u=2)
                     for h in range(2):
@@ -217,7 +210,7 @@ def tile_optimalnet_pa_t_kernel(tc, x, W1, b1, W2, b2, out_0, out_1, out_2):
                                 nc.tensor.transpose(
                                     bank[:, k * P : (k + 1) * P], w2words[:, 2 * h + tl, u, :], ident[:]
                                 )
-                        nc.vector.tensor_copy(
+                        nc.scalar.copy(
                             out=w2gw[:, 2 * h : 2 * h + 2, :, :],
                             in_=bank[:].rearrange("q (t u c) -> q t c u", t=2, u=2),
                         )
@@ -225,8 +218,7 @@ def tile_optimalnet_pa_t_kernel(tc, x, W1, b1, W2, b2, out_0, out_1, out_2):
                     nc.tensor.transpose(bank[:, 0:P], b2pad[:], ident[:])
                     nc.vector.tensor_copy(out=b2f[:], in_=bank[:, 0:4])
                     nc.vector.quantize_mx(out=w2q[:].bitcast(FP8X4), scales=w2s[:], in_=w2g[:])
-                    sbs[0] = spread_row_sums(0)
-            for c in range(1, 4):
+            for c in range(4):
                 sbs[c] = spread_row_sums(c)
 
         work = ctx.enter_context(tc.tile_pool(name="work", bufs=1))
@@ -279,7 +271,7 @@ def tile_optimalnet_pa_t_kernel(tc, x, W1, b1, W2, b2, out_0, out_1, out_2):
         def quantise_h(c):
             nc.vector.quantize_mx(out=hq[c][:].bitcast(FP8X4), scales=hs[c][:], in_=hg[c][:])
 
-        def layer2(t, c):
+        def product2(t, c):
             if t == 0:
                 v2[c] = keep.tile([P, 4 * CW], F32, name="v2_%d" % c, tag="hv%d" % c)
             z = pz.tile([P, CW], F32, name="z2", tag="z")
@@ -292,14 +284,10 @@ def tile_optimalnet_pa_t_kernel(tc, x, W1, b1, W2, b2, out_0, out_1, out_2):
                 start=True,
                 stop=True,
             )
-            nc.scalar.activation(
-                out=v2[c][:, t * CW : (t + 1) * CW],
-                in_=z[:],
-                func=FN.Relu,
-                bias=b2f[:, t : t + 1],
-                scale=1.0,
-                accum_out=acc2[:, t * CH + c : t * CH + c + 1],
-            )
+            return z
+
+        def exit2(t, c, z, on_vector=False):
+            relu_and_sum(on_vector, v2[c][:, t * CW : (t + 1) * CW], z, b2f[:, t : t + 1], acc2, t * CH + c)
 
         def sum_of_means():
             kb = pz.tile([P, CW], F32, name="kb", tag="z")
@@ -339,17 +327,24 @@ def tile_optimalnet_pa_t_kernel(tc, x, W1, b1, W2, b2, out_0, out_1, out_2):
                 sbs[c + 4] = spread_row_sums(c + 4)
             if c >= 2:
                 quantise_h(c - 2)
-                layer2(0, c - 2)
-                layer2(1, c - 2)
+                for t in range(2):
+                    exit2(t, c - 2, product2(t, c - 2))
             regroup(c)
             if c == 0:
                 sum_of_means()
             if c == 1:
                 store_m1()
-        for c in range(CH - 2, CH):
-            quantise_h(c)
-            layer2(0, c)
-            layer2(1, c)
+        quantise_h(CH - 2)
+        for t in range(2):
+            exit2(t, CH - 2, product2(t, CH - 2))
+        ahead = product2(2, 0)
+        quantise_h(CH - 1)
+        exit2(2, 0, ahead, True)
+        last = [product2(t, CH - 1) for t in range(2)]
+        exit2(0, CH - 1, last[0])
+        exit2(1, CH - 1, last[1], True)
+        for c in range(1, 4):
+            exit2(2, c, product2(2, c), True)
 
         def natural(h, j):
             bank = pt.tile([P, CW], F32, name="vn", tag="pt")
@@ -378,9 +373,10 @@ def tile_optimalnet_pa_t_kernel(tc, x, W1, b1, W2, b2, out_0, out_1, out_2):
 
         nc.vector.scalar_tensor_tensor(out=sh[:], in0=sx[:], scalar=k1[:, 0:1], in1=sv[:], op0=ALU.mult, op1=ALU.add)
 
+        means2(0)
+        rest = [(3, c) for c in range(4)] + [(t, c) for c in range(4, CH) for t in (2, 3)]
         for h in range(2):
             cols = slice(h * HALF, (h + 1) * HALF)
-            means2(h)
             if h == 1:
                 nc.sync.dma_start(out=out_2.rearrange("(o n) -> o n", o=1), in_=m2r[0:1, :])
             vn = {}
@@ -388,8 +384,10 @@ def tile_optimalnet_pa_t_kernel(tc, x, W1, b1, W2, b2, out_0, out_1, out_2):
                 vn[j] = natural(h, j)
             for c in range(CH):
                 if h == 0:
-                    layer2(2, c)
-                    layer2(3, c)
+                    for t, cc in rest[2 * c : 2 * c + 2]:
+                        exit2(t, cc, product2(t, cc))
+                    if c == CH - 2:
+                        means2(1)
                 ob = work.tile([P, 4, HALF], F32, name="ob", tag="ob", bufs=4)
                 for j in (2 * c, 2 * c + 1):
                     for k in range(2):

@@ -18,14 +18,13 @@ C = 0.01 * 0.001 / 1
 NT = ROWS // P
 CH = 8
 CW = 512
-HALF = D2 // 2
 FLOPS = 2 * ROWS * D0 * D1 + 2 * ROWS * D1 * D2
 
 
 def tile_optimalnet_pa_t_kernel(tc, x, W1, b1, W2, b2, out_0, out_1, out_2):
     nc = tc.nc
     x_v = x.rearrange("(p a) i -> p (a i)", a=NT)
-    out_v = out_0.rearrange("(p a) o -> p a o", a=NT)
+    out_v = out_0.rearrange("(p a) o -> p (a o)", a=NT)
 
     with ExitStack() as ctx:
         ctx.enter_context(tc.manual_schedule())
@@ -145,9 +144,10 @@ def tile_optimalnet_pa_t_kernel(tc, x, W1, b1, W2, b2, out_0, out_1, out_2):
             def row_sums_x(c):
                 for l in range(4):
                     a = 4 * c + l
+                    row = xn[c][:, l * D0 : (l + 1) * D0]
                     nc.vector.tensor_scalar(
                         out=jx[:],
-                        in0=xn[c][:, l * D0 : (l + 1) * D0],
+                        in0=row,
                         scalar1=1.0,
                         scalar2=None,
                         op0=ALU.mult,
@@ -183,7 +183,7 @@ def tile_optimalnet_pa_t_kernel(tc, x, W1, b1, W2, b2, out_0, out_1, out_2):
             nc.vector.tensor_copy(out=b2pad[0:4, :], in_=b2r[:])
             quantise_x(0)
             for t in range(4):
-                words_to_k(w1n[:].bitcast(F32), t * 512, w1g, t * P, t % 2 == 1)
+                words_to_k(w1n[:].bitcast(F32), t * 512, w1g, t * P, t in (1, 3))
             transpose_x(1)
             nc.vector.quantize_mx(out=w1q[:].bitcast(FP8X4), scales=w1s[:], in_=w1g[:])
 
@@ -191,7 +191,7 @@ def tile_optimalnet_pa_t_kernel(tc, x, W1, b1, W2, b2, out_0, out_1, out_2):
                 if c + 5 < CH:
                     load_x(c + 5, 1)
                 layer1(0, c)
-                layer1(1, c, c == CH - 1)
+                layer1(1, c)
                 layer1(2, c)
                 if c + 1 < CH:
                     quantise_x(c + 1)
@@ -199,7 +199,7 @@ def tile_optimalnet_pa_t_kernel(tc, x, W1, b1, W2, b2, out_0, out_1, out_2):
                     transpose_x(c + 2)
                 if c + 1 < CH:
                     row_sums_x(c + 1)
-                if c == 3:
+                if c == 5:
                     w2words = w2n[:].bitcast(F32).rearrange("p (t w u) -> p t u w", t=4, u=2)
                     w2gw = w2g[:].bitcast(F32).rearrange("q (t c u) -> q t c u", t=4, u=2)
                     for h in range(2):
@@ -263,17 +263,12 @@ def tile_optimalnet_pa_t_kernel(tc, x, W1, b1, W2, b2, out_0, out_1, out_2):
             hg[c] = work.tile([P, 4 * CW], BF16, name="hg", tag="hg", bufs=3, align_bytes=64)
             dst = hg[c][:].rearrange("p (c i t) -> p c t i", i=4, t=4)
             src = ht[c][:].rearrange("p (t c i) -> p c t i", t=4, i=4)
-            if c in (2, 4, 6):
-                nc.scalar.copy(out=dst, in_=src)
-            else:
-                nc.vector.tensor_copy(out=dst, in_=src)
+            nc.vector.tensor_copy(out=dst, in_=src)
 
         def quantise_h(c):
             nc.vector.quantize_mx(out=hq[c][:].bitcast(FP8X4), scales=hs[c][:], in_=hg[c][:])
 
         def product2(t, c):
-            if t == 0:
-                v2[c] = keep.tile([P, 4 * CW], F32, name="v2_%d" % c, tag="hv%d" % c)
             z = pz.tile([P, CW], F32, name="z2", tag="z")
             nc.tensor.matmul_mx(
                 out=z[:],
@@ -310,6 +305,9 @@ def tile_optimalnet_pa_t_kernel(tc, x, W1, b1, W2, b2, out_0, out_1, out_2):
             )
             nc.sync.dma_start(out=out_1.rearrange("(o n) -> o n", o=1), in_=m1r[0:1, :])
 
+        def new_v2(c):
+            v2[c] = keep.tile([P, 4 * CW], F32, name="v2_%d" % c, tag="hv%d" % c)
+
         LEAD = 3
         for t in range(3):
             scaled_mean1(t)
@@ -325,81 +323,76 @@ def tile_optimalnet_pa_t_kernel(tc, x, W1, b1, W2, b2, out_0, out_1, out_2):
             row_sums_v1(c)
             if c + 4 < CH:
                 sbs[c + 4] = spread_row_sums(c + 4)
-            if c >= 2:
-                quantise_h(c - 2)
-                for t in range(2):
-                    exit2(t, c - 2, product2(t, c - 2))
+            if c >= 1:
+                quantise_h(c - 1)
             regroup(c)
+            if c >= 1:
+                new_v2(c - 1)
+                for t in range(4):
+                    exit2(t, c - 1, product2(t, c - 1))
             if c == 0:
                 sum_of_means()
             if c == 1:
                 store_m1()
-        quantise_h(CH - 2)
-        for t in range(2):
-            exit2(t, CH - 2, product2(t, CH - 2))
-        ahead = product2(2, 0)
-        quantise_h(CH - 1)
-        exit2(2, 0, ahead, True)
-        last = [product2(t, CH - 1) for t in range(2)]
-        exit2(0, CH - 1, last[0])
-        exit2(1, CH - 1, last[1], True)
-        for c in range(1, 4):
-            exit2(2, c, product2(2, c), True)
+        tail = range(CH - 1, CH)
+        for c in tail:
+            quantise_h(c)
+            new_v2(c)
+        for c in tail:
+            last = [product2(t, c) for t in range(4)]
+            if c == CH - 1:
+                nc.vector.tensor_reduce(
+                    out=s2[:],
+                    in_=acc2[:].rearrange("p (t c) -> p t c", t=4)[:, :, 0 : CH - 1],
+                    axis=AXIS.X,
+                    op=ALU.add,
+                )
+            for t in range(4):
+                exit2(t, c, last[t], t in (2, 3))
 
-        def natural(h, j):
-            bank = pt.tile([P, CW], F32, name="vn", tag="pt")
-            for k in range(2):
-                a = 2 * j + k
-                for tl in range(2):
-                    first = (2 * h + tl) * CW + (a % 4) * P
-                    col = (2 * k + tl) * P
-                    nc.tensor.transpose(bank[:, col : col + P], v2[a // 4][:, first : first + P], ident[:])
+        def natural(a):
+            pool, tag = (pt, "pt") if a % 8 < 4 else (pz, "z")
+            bank = pool.tile([P, CW], F32, name="vn", tag=tag)
+            for t in range(4):
+                first = t * CW + (a % 4) * P
+                nc.tensor.transpose(bank[:, t * P : (t + 1) * P], v2[a // 4][:, first : first + P], ident[:])
             return bank
 
-        def means2(h):
-            cols = slice(h * HALF, (h + 1) * HALF)
-            nc.vector.tensor_reduce(
-                out=s2[:, 2 * h : 2 * h + 2],
-                in_=acc2[:, 16 * h : 16 * h + 16].rearrange("p (t c) -> p t c", t=2),
-                axis=AXIS.X,
-                op=ALU.add,
-            )
-            mb = pz.tile([P, CW], F32, name="mb", tag="z")
-            for tl in range(2):
-                t = 2 * h + tl
-                nc.tensor.transpose(mb[:, tl * P : (tl + 1) * P], s2[:, t : t + 1].to_broadcast([P, P]), ident[:])
-            nc.scalar.activation(out=cm2b[:, cols], in_=mb[:, 0:HALF], func=FN.Copy, scale=C / ROWS)
-            nc.scalar.activation(out=m2r[0:32, cols], in_=mb[0:32, 0:HALF], func=FN.Copy, scale=1.0 / ROWS)
-
         nc.vector.scalar_tensor_tensor(out=sh[:], in0=sx[:], scalar=k1[:, 0:1], in1=sv[:], op0=ALU.mult, op1=ALU.add)
+        AHEAD = 6
+        vn = {}
+        for a in range(AHEAD - 1):
+            vn[a] = natural(a)
+        mb = pz.tile([P, CW], F32, name="mb", tag="z")
+        for t in range(4):
+            for k, part in enumerate((s2[:, t : t + 1], acc2[:, t * CH + CH - 1 : t * CH + CH])):
+                nc.tensor.matmul(
+                    out=mb[:, t * P : (t + 1) * P],
+                    lhsT=part.to_broadcast([P, P]),
+                    rhs=ident[:],
+                    is_transpose=True,
+                    start=(k == 0),
+                    stop=(k == 1),
+                )
+        nc.scalar.activation(out=cm2b[:, 0:256], in_=mb[:, 0:256], func=FN.Copy, scale=C / ROWS)
+        nc.vector.tensor_scalar(out=cm2b[:, 256:512], in0=mb[:, 256:512], scalar1=C / ROWS, scalar2=None, op0=ALU.mult)
+        nc.scalar.activation(out=m2r[0:32, :], in_=mb[0:32, :], func=FN.Copy, scale=1.0 / ROWS)
+        nc.sync.dma_start(out=out_2.rearrange("(o n) -> o n", o=1), in_=m2r[0:1, :])
+        vn[AHEAD - 1] = natural(AHEAD - 1)
 
-        means2(0)
-        rest = [(3, c) for c in range(4)] + [(t, c) for c in range(4, CH) for t in (2, 3)]
-        for h in range(2):
-            cols = slice(h * HALF, (h + 1) * HALF)
-            if h == 1:
-                nc.sync.dma_start(out=out_2.rearrange("(o n) -> o n", o=1), in_=m2r[0:1, :])
-            vn = {}
-            for j in range(4):
-                vn[j] = natural(h, j)
-            for c in range(CH):
-                if h == 0:
-                    for t, cc in rest[2 * c : 2 * c + 2]:
-                        exit2(t, cc, product2(t, cc))
-                    if c == CH - 2:
-                        means2(1)
-                ob = work.tile([P, 4, HALF], F32, name="ob", tag="ob", bufs=4)
-                for j in (2 * c, 2 * c + 1):
-                    for k in range(2):
-                        a = 2 * j + k
-                        nc.vector.scalar_tensor_tensor(
-                            out=ob[:, a % 4, :],
-                            in0=cm2b[:, cols],
-                            scalar=sh[:, a : a + 1],
-                            in1=vn[j][:, k * HALF : (k + 1) * HALF],
-                            op0=ALU.mult,
-                            op1=ALU.add,
-                        )
-                    if j + 4 < NT // 2:
-                        vn[j + 4] = natural(h, j + 4)
-                nc.sync.dma_start(out=out_v[:, 4 * c : 4 * c + 4, cols], in_=ob[:])
+        ob = None
+        for a in range(NT):
+            if a % 2 == 0:
+                ob = work.tile([P, 2 * D2], F32, name="ob", tag="ob", bufs=4)
+            nc.vector.scalar_tensor_tensor(
+                out=ob[:, (a % 2) * D2 : (a % 2 + 1) * D2],
+                in0=cm2b[:],
+                scalar=sh[:, a : a + 1],
+                in1=vn[a][:],
+                op0=ALU.mult,
+                op1=ALU.add,
+            )
+            if a % 2 == 1:
+                nc.sync.dma_start(out=out_v[:, (a - 1) * D2 : (a + 1) * D2], in_=ob[:])
+            if a + AHEAD < NT:
+                vn[a + AHEAD] = natural(a + AHEAD)

@@ -29,8 +29,7 @@ def tile_optimalnet_pa_t_kernel(tc, x, W1, b1, W2, b2, out_0, out_1, out_2):
     with ExitStack() as ctx:
         ctx.enter_context(tc.manual_schedule())
         keep = ctx.enter_context(tc.tile_pool(name="keep", bufs=1))
-        pt = ctx.enter_context(tc.psum_pool(name="pt", bufs=4))
-        pz = ctx.enter_context(tc.psum_pool(name="pz", bufs=4))
+        banks = {}
 
         hv = [keep.tile([P, 4 * CW], F32, name="hv%d" % c) for c in range(CH)]
         xq = [keep.tile([P, 2 * CW], U32, name="xq%d" % c, align_bytes=64) for c in range(CH)]
@@ -64,7 +63,7 @@ def tile_optimalnet_pa_t_kernel(tc, x, W1, b1, W2, b2, out_0, out_1, out_2):
         nc.gpsimd.memset(zeros[:], 0.0)
 
         def spread_row_sums(c):
-            sb = pt.tile([P, CW], F32, name="sb", tag="pt")
+            sb = banks["pt"].tile([P, CW], F32, name="sb", tag="pt")
             for l in range(4):
                 a = 4 * c + l
                 nc.tensor.transpose(sb[:, l * P : (l + 1) * P], sx[:, a : a + 1].to_broadcast([P, P]), ident[:])
@@ -80,7 +79,7 @@ def tile_optimalnet_pa_t_kernel(tc, x, W1, b1, W2, b2, out_0, out_1, out_2):
                 nc.scalar.activation(out=v, in_=z[:], func=FN.Relu, bias=bias, scale=1.0, accum_out=total)
 
         def layer1(t, c, on_vector=False):
-            z = pz.tile([P, CW], F32, name="z", tag="z")
+            z = banks["pz"].tile([P, CW], F32, name="z", tag="z")
             for g in range(2):
                 wcols = slice(g * 512 + t * P, g * 512 + (t + 1) * P)
                 xcols = slice(g * CW, (g + 1) * CW)
@@ -107,7 +106,9 @@ def tile_optimalnet_pa_t_kernel(tc, x, W1, b1, W2, b2, out_0, out_1, out_2):
             )
 
         sbs = {}
-        with tc.tile_pool(name="stage", bufs=1) as stage:
+        with tc.tile_pool(name="stage", bufs=1) as stage, ExitStack() as first_banks:
+            banks["pt"] = first_banks.enter_context(tc.psum_pool(name="pt", bufs=4))
+            banks["pz"] = first_banks.enter_context(tc.psum_pool(name="pz", bufs=4))
             xn = {}
             xg = {}
 
@@ -121,7 +122,7 @@ def tile_optimalnet_pa_t_kernel(tc, x, W1, b1, W2, b2, out_0, out_1, out_2):
                 xn[c] = xt
 
             def words_to_k(words, first, grouped, col0, on_vector):
-                bank = pt.tile([P, CW], F32, name="xt", tag="pt")
+                bank = banks["pt"].tile([P, CW], F32, name="xt", tag="pt")
                 for g in range(2):
                     for u in range(2):
                         b = 2 * g + u
@@ -158,6 +159,26 @@ def tile_optimalnet_pa_t_kernel(tc, x, W1, b1, W2, b2, out_0, out_1, out_2):
             def quantise_x(c):
                 nc.vector.quantize_mx(out=xq[c][:].bitcast(FP8X4), scales=xs[c][:], in_=xg[c][:])
 
+            def prepare_w2():
+                w2words = w2n[:].bitcast(F32).rearrange("p (t w u) -> p t u w", t=4, u=2)
+                w2gw = w2g[:].bitcast(F32).rearrange("q (t c u) -> q t c u", t=4, u=2)
+                for h in range(2):
+                    bank = banks["pt"].tile([P, CW], F32, name="w2t", tag="pt")
+                    for tl in range(2):
+                        for u in range(2):
+                            k = tl * 2 + u
+                            nc.tensor.transpose(
+                                bank[:, k * P : (k + 1) * P], w2words[:, 2 * h + tl, u, :], ident[:]
+                            )
+                    nc.scalar.copy(
+                        out=w2gw[:, 2 * h : 2 * h + 2, :, :],
+                        in_=bank[:].rearrange("q (t u c) -> q t c u", t=2, u=2),
+                    )
+                bank = banks["pt"].tile([P, CW], F32, name="b2t", tag="pt")
+                nc.tensor.transpose(bank[:, 0:P], b2pad[:], ident[:])
+                nc.vector.tensor_copy(out=b2f[:], in_=bank[:, 0:4])
+                nc.vector.quantize_mx(out=w2q[:].bitcast(FP8X4), scales=w2s[:], in_=w2g[:])
+
             w1n = stage.tile([P, 4 * D0], BF16, name="w1n")
             w1g = stage.tile([P, 4 * D0], BF16, name="w1g", align_bytes=64)
             w2n = stage.tile([P, 4 * D1], BF16, name="w2n")
@@ -190,38 +211,23 @@ def tile_optimalnet_pa_t_kernel(tc, x, W1, b1, W2, b2, out_0, out_1, out_2):
             for c in range(CH):
                 if c + 5 < CH:
                     load_x(c + 5, 1)
-                layer1(0, c)
-                layer1(1, c)
-                layer1(2, c)
+                for t in range(3):
+                    layer1(t, c)
                 if c + 1 < CH:
                     quantise_x(c + 1)
                 if c + 2 < CH:
                     transpose_x(c + 2)
                 if c + 1 < CH:
                     row_sums_x(c + 1)
-                if c == 5:
-                    w2words = w2n[:].bitcast(F32).rearrange("p (t w u) -> p t u w", t=4, u=2)
-                    w2gw = w2g[:].bitcast(F32).rearrange("q (t c u) -> q t c u", t=4, u=2)
-                    for h in range(2):
-                        bank = pt.tile([P, CW], F32, name="w2t", tag="pt")
-                        for tl in range(2):
-                            for u in range(2):
-                                k = tl * 2 + u
-                                nc.tensor.transpose(
-                                    bank[:, k * P : (k + 1) * P], w2words[:, 2 * h + tl, u, :], ident[:]
-                                )
-                        nc.scalar.copy(
-                            out=w2gw[:, 2 * h : 2 * h + 2, :, :],
-                            in_=bank[:].rearrange("q (t u c) -> q t c u", t=2, u=2),
-                        )
-                    bank = pt.tile([P, CW], F32, name="b2t", tag="pt")
-                    nc.tensor.transpose(bank[:, 0:P], b2pad[:], ident[:])
-                    nc.vector.tensor_copy(out=b2f[:], in_=bank[:, 0:4])
-                    nc.vector.quantize_mx(out=w2q[:].bitcast(FP8X4), scales=w2s[:], in_=w2g[:])
-            for c in range(4):
-                sbs[c] = spread_row_sums(c)
+                if c == 6:
+                    prepare_w2()
 
         work = ctx.enter_context(tc.tile_pool(name="work", bufs=1))
+        banks["pt"] = ctx.enter_context(tc.psum_pool(name="ps", bufs=3))
+        banks["pz"] = ctx.enter_context(tc.psum_pool(name="pm", bufs=4))
+        banks["pv"] = ctx.enter_context(tc.psum_pool(name="pv", bufs=1))
+        for c in range(3):
+            sbs[c] = spread_row_sums(c)
         hq = [work.tile([P, CW], U32, name="hq%d" % c, align_bytes=64) for c in range(CH)]
         hs = [work.tile([P, CW], U8, name="hs%d" % c, align_bytes=64) for c in range(CH)]
         ht = {}
@@ -242,7 +248,7 @@ def tile_optimalnet_pa_t_kernel(tc, x, W1, b1, W2, b2, out_0, out_1, out_2):
             )
 
         def row_sums_v1(c):
-            bank = pz.tile([P, CW], F32, name="svb", tag="z")
+            bank = banks["pv"].tile([P, CW], F32, name="svb", tag="v")
             for l in range(4):
                 for t in range(4):
                     nc.tensor.matmul(
@@ -269,7 +275,7 @@ def tile_optimalnet_pa_t_kernel(tc, x, W1, b1, W2, b2, out_0, out_1, out_2):
             nc.vector.quantize_mx(out=hq[c][:].bitcast(FP8X4), scales=hs[c][:], in_=hg[c][:])
 
         def product2(t, c):
-            z = pz.tile([P, CW], F32, name="z2", tag="z")
+            z = banks["pz"].tile([P, CW], F32, name="z2", tag="z")
             nc.tensor.matmul_mx(
                 out=z[:],
                 lhsT=w2q[:, t * P : (t + 1) * P].bitcast(FP8X4),
@@ -285,7 +291,7 @@ def tile_optimalnet_pa_t_kernel(tc, x, W1, b1, W2, b2, out_0, out_1, out_2):
             relu_and_sum(on_vector, v2[c][:, t * CW : (t + 1) * CW], z, b2f[:, t : t + 1], acc2, t * CH + c)
 
         def sum_of_means():
-            kb = pz.tile([P, CW], F32, name="kb", tag="z")
+            kb = banks["pz"].tile([P, CW], F32, name="kb", tag="z")
             for t in range(4):
                 nc.tensor.transpose(kb[:, t * P : (t + 1) * P], cm1[:, t : t + 1].to_broadcast([P, P]), ident[:])
             nc.scalar.activation(out=ja[:], in_=kb[:], func=FN.Copy, accum_out=k1[:, 0:1])
@@ -294,7 +300,7 @@ def tile_optimalnet_pa_t_kernel(tc, x, W1, b1, W2, b2, out_0, out_1, out_2):
             nc.vector.tensor_reduce(
                 out=s1[:], in_=acc1[:].rearrange("p (t c) -> p t c", t=4), axis=AXIS.X, op=ALU.add
             )
-            m1b = pz.tile([P, CW], F32, name="m1b", tag="z")
+            m1b = banks["pz"].tile([P, CW], F32, name="m1b", tag="z")
             for t in range(4):
                 nc.tensor.transpose(m1b[:, t * P : (t + 1) * P], s1[:, t : t + 1].to_broadcast([P, P]), ident[:])
             nc.scalar.activation(
@@ -307,6 +313,14 @@ def tile_optimalnet_pa_t_kernel(tc, x, W1, b1, W2, b2, out_0, out_1, out_2):
 
         def new_v2(c):
             v2[c] = keep.tile([P, 4 * CW], F32, name="v2_%d" % c, tag="hv%d" % c)
+
+        def natural(a):
+            pool, tag = (banks["pt"], "pt") if a % 7 < 3 else (banks["pz"], "z")
+            bank = pool.tile([P, CW], F32, name="vn", tag=tag)
+            for t in range(4):
+                first = t * CW + (a % 4) * P
+                nc.tensor.transpose(bank[:, t * P : (t + 1) * P], v2[a // 4][:, first : first + P], ident[:])
+            return bank
 
         LEAD = 3
         for t in range(3):
@@ -321,8 +335,8 @@ def tile_optimalnet_pa_t_kernel(tc, x, W1, b1, W2, b2, out_0, out_1, out_2):
             for t in range(3 if c < LEAD else 0, 4):
                 correct(t, c)
             row_sums_v1(c)
-            if c + 4 < CH:
-                sbs[c + 4] = spread_row_sums(c + 4)
+            if c + 3 < CH:
+                sbs[c + 3] = spread_row_sums(c + 3)
             if c >= 1:
                 quantise_h(c - 1)
             regroup(c)
@@ -330,40 +344,30 @@ def tile_optimalnet_pa_t_kernel(tc, x, W1, b1, W2, b2, out_0, out_1, out_2):
                 new_v2(c - 1)
                 for t in range(4):
                     exit2(t, c - 1, product2(t, c - 1))
-            if c == 0:
+            if c == 2:
                 sum_of_means()
-            if c == 1:
+            if c == 3:
                 store_m1()
-        tail = range(CH - 1, CH)
-        for c in tail:
-            quantise_h(c)
-            new_v2(c)
-        for c in tail:
-            last = [product2(t, c) for t in range(4)]
-            if c == CH - 1:
-                nc.vector.tensor_reduce(
-                    out=s2[:],
-                    in_=acc2[:].rearrange("p (t c) -> p t c", t=4)[:, :, 0 : CH - 1],
-                    axis=AXIS.X,
-                    op=ALU.add,
-                )
-            for t in range(4):
-                exit2(t, c, last[t], t in (2, 3))
-
-        def natural(a):
-            pool, tag = (pt, "pt") if a % 8 < 4 else (pz, "z")
-            bank = pool.tile([P, CW], F32, name="vn", tag=tag)
-            for t in range(4):
-                first = t * CW + (a % 4) * P
-                nc.tensor.transpose(bank[:, t * P : (t + 1) * P], v2[a // 4][:, first : first + P], ident[:])
-            return bank
+        vn = {}
+        for a in range(3):
+            vn[a] = natural(a)
+        quantise_h(CH - 1)
+        new_v2(CH - 1)
+        last = [product2(t, CH - 1) for t in range(4)]
+        nc.vector.tensor_reduce(
+            out=s2[:],
+            in_=acc2[:].rearrange("p (t c) -> p t c", t=4)[:, :, 0 : CH - 1],
+            axis=AXIS.X,
+            op=ALU.add,
+        )
+        for t in range(4):
+            exit2(t, CH - 1, last[t], t >= 2)
 
         nc.vector.scalar_tensor_tensor(out=sh[:], in0=sx[:], scalar=k1[:, 0:1], in1=sv[:], op0=ALU.mult, op1=ALU.add)
         AHEAD = 6
-        vn = {}
-        for a in range(AHEAD - 1):
+        for a in range(3, AHEAD - 1):
             vn[a] = natural(a)
-        mb = pz.tile([P, CW], F32, name="mb", tag="z")
+        mb = banks["pv"].tile([P, CW], F32, name="mb", tag="v")
         for t in range(4):
             for k, part in enumerate((s2[:, t : t + 1], acc2[:, t * CH + CH - 1 : t * CH + CH])):
                 nc.tensor.matmul(

@@ -18,6 +18,7 @@ C = 0.01 * 0.001 / 1
 NT = ROWS // P
 CH = 8
 CW = 512
+EARLY = 4
 FLOPS = 2 * ROWS * D0 * D1 + 2 * ROWS * D1 * D2
 
 
@@ -269,7 +270,19 @@ def tile_optimalnet_pa_t_kernel(tc, x, W1, b1, W2, b2, out_0, out_1, out_2):
             hg[c] = work.tile([P, 4 * CW], BF16, name="hg", tag="hg", bufs=3, align_bytes=64)
             dst = hg[c][:].rearrange("p (c i t) -> p c t i", i=4, t=4)
             src = ht[c][:].rearrange("p (t c i) -> p c t i", t=4, i=4)
-            nc.vector.tensor_copy(out=dst, in_=src)
+            if c in (0, 1, CH - 1):
+                nc.vector.tensor_copy(out=dst, in_=src)
+            else:
+                for i in range(4):
+                    part = slice(i * 32, (i + 1) * 32)
+                    nc.gpsimd.tensor_scalar(
+                        out=dst[:, part, :, :],
+                        in0=src[:, part, :, :],
+                        scalar1=1.0,
+                        scalar2=0.0,
+                        op0=ALU.mult,
+                        op1=ALU.add,
+                    )
 
         def quantise_h(c):
             nc.vector.quantize_mx(out=hq[c][:].bitcast(FP8X4), scales=hs[c][:], in_=hg[c][:])
@@ -312,7 +325,16 @@ def tile_optimalnet_pa_t_kernel(tc, x, W1, b1, W2, b2, out_0, out_1, out_2):
             nc.sync.dma_start(out=out_1.rearrange("(o n) -> o n", o=1), in_=m1r[0:1, :])
 
         def new_v2(c):
-            v2[c] = keep.tile([P, 4 * CW], F32, name="v2_%d" % c, tag="hv%d" % c)
+            if c < EARLY:
+                v2[c] = keep.tile([P, 4 * CW], F32, name="v2_%d" % c, tag="hv%d" % c)
+            else:
+                v2[c] = work.tile([P, 4 * CW], F32, name="v2_%d" % c)
+
+        def row_sums_h(first, last):
+            cols = slice(4 * first, 4 * last)
+            nc.vector.scalar_tensor_tensor(
+                out=sh[:, cols], in0=sx[:, cols], scalar=k1[:, 0:1], in1=sv[:, cols], op0=ALU.mult, op1=ALU.add
+            )
 
         def natural(a):
             pool, tag = (banks["pt"], "pt") if a % 7 < 3 else (banks["pz"], "z")
@@ -334,7 +356,8 @@ def tile_optimalnet_pa_t_kernel(tc, x, W1, b1, W2, b2, out_0, out_1, out_2):
         for c in range(CH):
             for t in range(3 if c < LEAD else 0, 4):
                 correct(t, c)
-            row_sums_v1(c)
+            if c < EARLY:
+                row_sums_v1(c)
             if c + 3 < CH:
                 sbs[c + 3] = spread_row_sums(c + 3)
             if c >= 1:
@@ -363,7 +386,7 @@ def tile_optimalnet_pa_t_kernel(tc, x, W1, b1, W2, b2, out_0, out_1, out_2):
         for t in range(4):
             exit2(t, CH - 1, last[t], t >= 2)
 
-        nc.vector.scalar_tensor_tensor(out=sh[:], in0=sx[:], scalar=k1[:, 0:1], in1=sv[:], op0=ALU.mult, op1=ALU.add)
+        row_sums_h(0, EARLY)
         AHEAD = 6
         for a in range(3, AHEAD - 1):
             vn[a] = natural(a)
@@ -388,6 +411,8 @@ def tile_optimalnet_pa_t_kernel(tc, x, W1, b1, W2, b2, out_0, out_1, out_2):
         for a in range(NT):
             if a % 2 == 0:
                 ob = work.tile([P, 2 * D2], F32, name="ob", tag="ob", bufs=4)
+            if a % 4 == 0 and a >= 4 * EARLY:
+                row_sums_h(a // 4, a // 4 + 1)
             nc.vector.scalar_tensor_tensor(
                 out=ob[:, (a % 2) * D2 : (a % 2 + 1) * D2],
                 in0=cm2b[:],
@@ -400,3 +425,5 @@ def tile_optimalnet_pa_t_kernel(tc, x, W1, b1, W2, b2, out_0, out_1, out_2):
                 nc.sync.dma_start(out=out_v[:, (a - 1) * D2 : (a + 1) * D2], in_=ob[:])
             if a + AHEAD < NT:
                 vn[a + AHEAD] = natural(a + AHEAD)
+            if a % 4 == 2 and a < 4 * (CH - EARLY):
+                row_sums_v1(EARLY + a // 4)

@@ -191,7 +191,10 @@ def tile_optimalnet_pa_t_kernel(tc, x, W1, b1, W2, b2, out_0, out_1, out_2):
             nc.sync.dma_start(out=b1r[:], in_=b1.rearrange("(p t) -> p t", t=4))
             nc.sync.dma_start(out=b2r[:], in_=b2.rearrange("(t p) -> t p", p=P))
             load_x(0, 4)
-            nc.sync.dma_start(out=w1n[:], in_=W1.rearrange("(p t) i -> p (t i)", t=4))
+            for t in range(4):
+                nc.sync.dma_start(
+                    out=w1n[:, t * D0 : (t + 1) * D0], in_=W1.rearrange("(p t) i -> p (t i)", t=4)[:, t * D0 : (t + 1) * D0]
+                )
             for c in range(1, 5):
                 load_x(c, 1)
             nc.sync.dma_start(
@@ -273,11 +276,13 @@ def tile_optimalnet_pa_t_kernel(tc, x, W1, b1, W2, b2, out_0, out_1, out_2):
             if c in (0, 1, CH - 1):
                 nc.vector.tensor_copy(out=dst, in_=src)
             else:
+                whole = hg[c][:].rearrange("p (c t) -> p c t", t=4)
+                tiles = ht[c][:].rearrange("p (t c) -> p c t", t=4)
                 for i in range(4):
-                    part = slice(i * 32, (i + 1) * 32)
+                    part = slice(i * P, (i + 1) * P)
                     nc.gpsimd.tensor_scalar(
-                        out=dst[:, part, :, :],
-                        in0=src[:, part, :, :],
+                        out=whole[:, part, :],
+                        in0=tiles[:, part, :],
                         scalar1=1.0,
                         scalar2=0.0,
                         op0=ALU.mult,
@@ -388,8 +393,6 @@ def tile_optimalnet_pa_t_kernel(tc, x, W1, b1, W2, b2, out_0, out_1, out_2):
 
         row_sums_h(0, EARLY)
         AHEAD = 6
-        for a in range(3, AHEAD - 1):
-            vn[a] = natural(a)
         mb = banks["pv"].tile([P, CW], F32, name="mb", tag="v")
         for t in range(4):
             for k, part in enumerate((s2[:, t : t + 1], acc2[:, t * CH + CH - 1 : t * CH + CH])):
@@ -405,7 +408,8 @@ def tile_optimalnet_pa_t_kernel(tc, x, W1, b1, W2, b2, out_0, out_1, out_2):
         nc.vector.tensor_scalar(out=cm2b[:, 256:512], in0=mb[:, 256:512], scalar1=C / ROWS, scalar2=None, op0=ALU.mult)
         nc.scalar.activation(out=m2r[0:32, :], in_=mb[0:32, :], func=FN.Copy, scale=1.0 / ROWS)
         nc.sync.dma_start(out=out_2.rearrange("(o n) -> o n", o=1), in_=m2r[0:1, :])
-        vn[AHEAD - 1] = natural(AHEAD - 1)
+        for a in range(3, AHEAD):
+            vn[a] = natural(a)
 
         ob = None
         for a in range(NT):

@@ -18,7 +18,7 @@ C = 0.01 * 0.001 / 1
 NT = ROWS // P
 CH = 8
 CW = 512
-EARLY = 4
+EARLY = 6
 FLOPS = 2 * ROWS * D0 * D1 + 2 * ROWS * D1 * D2
 
 
@@ -35,6 +35,7 @@ def tile_optimalnet_pa_t_kernel(tc, x, W1, b1, W2, b2, out_0, out_1, out_2):
         hv = [keep.tile([P, 4 * CW], F32, name="hv%d" % c) for c in range(CH)]
         xq = [keep.tile([P, 2 * CW], U32, name="xq%d" % c, align_bytes=64) for c in range(CH)]
         xs = [keep.tile([P, 2 * CW], U8, name="xs%d" % c, align_bytes=64) for c in range(CH)]
+        vs = [keep.tile([P, CW], F32, name="vs%d" % c) for c in range(CH)]
         w1q = keep.tile([P, 1024], U32, name="w1q", align_bytes=64)
         w1s = keep.tile([P, 1024], U8, name="w1s", align_bytes=64)
         w2q = keep.tile([P, 512], U32, name="w2q", align_bytes=64)
@@ -94,6 +95,10 @@ def tile_optimalnet_pa_t_kernel(tc, x, W1, b1, W2, b2, out_0, out_1, out_2):
                     stop=(g == 1),
                 )
             relu_and_sum(on_vector, hv[c][:, t * CW : (t + 1) * CW], z, b1f[:, t : t + 1], acc1, t * CH + c)
+
+        def add_v1(c):
+            nc.gpsimd.tensor_tensor(out=vs[c][:], in0=hv[c][:, 0:CW], in1=hv[c][:, CW : 2 * CW], op=ALU.add)
+            nc.gpsimd.tensor_tensor(out=vs[c][:], in0=vs[c][:], in1=hv[c][:, 2 * CW : 3 * CW], op=ALU.add)
 
         def scaled_mean1(t):
             nc.vector.tensor_scalar(
@@ -217,6 +222,7 @@ def tile_optimalnet_pa_t_kernel(tc, x, W1, b1, W2, b2, out_0, out_1, out_2):
                     load_x(c + 5, 1)
                 for t in range(3):
                     layer1(t, c)
+                add_v1(c)
                 if c + 1 < CH:
                     quantise_x(c + 1)
                 if c + 2 < CH:
@@ -232,15 +238,15 @@ def tile_optimalnet_pa_t_kernel(tc, x, W1, b1, W2, b2, out_0, out_1, out_2):
         banks["pv"] = ctx.enter_context(tc.psum_pool(name="pv", bufs=1))
         for c in range(3):
             sbs[c] = spread_row_sums(c)
-        hq = [work.tile([P, CW], U32, name="hq%d" % c, align_bytes=64) for c in range(CH)]
-        hs = [work.tile([P, CW], U8, name="hs%d" % c, align_bytes=64) for c in range(CH)]
+        hq = {}
+        hs = {}
         ht = {}
         hg = {}
         v2 = {}
 
         def correct(t, c):
             if t == 0:
-                ht[c] = work.tile([P, 4 * CW], BF16, name="ht", tag="ht", bufs=6)
+                ht[c] = work.tile([P, 4 * CW], BF16, name="ht", tag="ht", bufs=5)
             seg = slice(t * CW, (t + 1) * CW)
             nc.vector.scalar_tensor_tensor(
                 out=ht[c][:, seg],
@@ -254,14 +260,14 @@ def tile_optimalnet_pa_t_kernel(tc, x, W1, b1, W2, b2, out_0, out_1, out_2):
         def row_sums_v1(c):
             bank = banks["pv"].tile([P, CW], F32, name="svb", tag="v")
             for l in range(4):
-                for t in range(4):
+                for k, part in enumerate((vs[c][:, l * P : (l + 1) * P], hv[c][:, 3 * CW + l * P : 3 * CW + (l + 1) * P])):
                     nc.tensor.matmul(
                         out=bank[:, l * P : (l + 1) * P],
-                        lhsT=hv[c][:, t * CW + l * P : t * CW + (l + 1) * P],
+                        lhsT=part,
                         rhs=ident[:],
                         is_transpose=True,
-                        start=(t == 0),
-                        stop=(t == 3),
+                        start=(k == 0),
+                        stop=(k == 1),
                     )
             for l in range(4):
                 a = 4 * c + l
@@ -290,10 +296,13 @@ def tile_optimalnet_pa_t_kernel(tc, x, W1, b1, W2, b2, out_0, out_1, out_2):
                     )
 
         def quantise_h(c):
+            hq[c] = work.tile([P, CW], U32, name="hq", tag="hq", bufs=3, align_bytes=64)
+            hs[c] = work.tile([P, CW], U8, name="hs", tag="hs", bufs=3, align_bytes=64)
             nc.vector.quantize_mx(out=hq[c][:].bitcast(FP8X4), scales=hs[c][:], in_=hg[c][:])
 
-        def product2(t, c):
-            z = banks["pz"].tile([P, CW], F32, name="z2", tag="z")
+        def product2(t, c, in_ps=False):
+            pool, tag = (banks["pt"], "pt") if in_ps else (banks["pz"], "z")
+            z = pool.tile([P, CW], F32, name="z2", tag=tag)
             nc.tensor.matmul_mx(
                 out=z[:],
                 lhsT=w2q[:, t * P : (t + 1) * P].bitcast(FP8X4),
@@ -342,7 +351,7 @@ def tile_optimalnet_pa_t_kernel(tc, x, W1, b1, W2, b2, out_0, out_1, out_2):
             )
 
         def natural(a):
-            pool, tag = (banks["pt"], "pt") if a % 7 < 3 else (banks["pz"], "z")
+            pool, tag = (banks["pt"], "pt") if a >= 3 and (a - 3) % 7 < 3 else (banks["pz"], "z")
             bank = pool.tile([P, CW], F32, name="vn", tag=tag)
             for t in range(4):
                 first = t * CW + (a % 4) * P
@@ -377,32 +386,33 @@ def tile_optimalnet_pa_t_kernel(tc, x, W1, b1, W2, b2, out_0, out_1, out_2):
             if c == 3:
                 store_m1()
         vn = {}
-        for a in range(3):
-            vn[a] = natural(a)
-        quantise_h(CH - 1)
-        new_v2(CH - 1)
-        last = [product2(t, CH - 1) for t in range(4)]
         nc.vector.tensor_reduce(
             out=s2[:],
-            in_=acc2[:].rearrange("p (t c) -> p t c", t=4)[:, :, 0 : CH - 1],
+            in_=acc2[:].rearrange("p (t c) -> p t c", t=4)[:, :, 0 : CH - 2],
             axis=AXIS.X,
             op=ALU.add,
         )
+        quantise_h(CH - 1)
+        new_v2(CH - 1)
+        last = [product2(t, CH - 1, t < 3) for t in range(4)]
+        for a in range(3):
+            vn[a] = natural(a)
         for t in range(4):
-            exit2(t, CH - 1, last[t], t >= 2)
+            exit2(t, CH - 1, last[t], t in (0, 1, 2))
 
         row_sums_h(0, EARLY)
         AHEAD = 6
         mb = banks["pv"].tile([P, CW], F32, name="mb", tag="v")
         for t in range(4):
-            for k, part in enumerate((s2[:, t : t + 1], acc2[:, t * CH + CH - 1 : t * CH + CH])):
+            n = t * CH + CH
+            for k, part in enumerate((s2[:, t : t + 1], acc2[:, n - 2 : n - 1], acc2[:, n - 1 : n])):
                 nc.tensor.matmul(
                     out=mb[:, t * P : (t + 1) * P],
                     lhsT=part.to_broadcast([P, P]),
                     rhs=ident[:],
                     is_transpose=True,
                     start=(k == 0),
-                    stop=(k == 1),
+                    stop=(k == 2),
                 )
         nc.scalar.activation(out=cm2b[:, 0:256], in_=mb[:, 0:256], func=FN.Copy, scale=C / ROWS)
         nc.vector.tensor_scalar(out=cm2b[:, 256:512], in0=mb[:, 256:512], scalar1=C / ROWS, scalar2=None, op0=ALU.mult)
@@ -414,7 +424,7 @@ def tile_optimalnet_pa_t_kernel(tc, x, W1, b1, W2, b2, out_0, out_1, out_2):
         ob = None
         for a in range(NT):
             if a % 2 == 0:
-                ob = work.tile([P, 2 * D2], F32, name="ob", tag="ob", bufs=4)
+                ob = work.tile([P, 2 * D2], F32, name="ob", tag="ob", bufs=8)
             if a % 4 == 0 and a >= 4 * EARLY:
                 row_sums_h(a // 4, a // 4 + 1)
             nc.vector.scalar_tensor_tensor(

from contextlib import ExitStack

import concourse.mybir as mybir
from concourse.masks import make_identity

F32 = mybir.dt.float32
BF16 = mybir.dt.bfloat16
U32 = mybir.dt.uint32
U8 = mybir.dt.uint8
FP8X4 = mybir.dt.float8_e4m3fn_x4
ALU = mybir.AluOpType
FN = mybir.ActivationFunctionType
AXIS = mybir.AxisListType

P = 128
ROWS, D0, D1, D2 = 4096, 1024, 512, 512
C = 0.01 * 0.001 / 1
NT = ROWS // P
CH = 8
CW = 512
EARLY = 6
FLOPS = 2 * ROWS * D0 * D1 + 2 * ROWS * D1 * D2


def tile_optimalnet_pa_t_kernel(tc, x, W1, b1, W2, b2, out_0, out_1, out_2):
    nc = tc.nc
    x_v = x.rearrange("(p a) i -> p (a i)", a=NT)
    out_v = out_0.rearrange("(p a) o -> p (a o)", a=NT)

    with ExitStack() as ctx:
        ctx.enter_context(tc.manual_schedule())
        keep = ctx.enter_context(tc.tile_pool(name="keep", bufs=1))
        banks = {}

        hv = [keep.tile([P, 4 * CW], F32, name="hv%d" % c) for c in range(CH)]
        xq = [keep.tile([P, 2 * CW], U32, name="xq%d" % c, align_bytes=64) for c in range(CH)]
        xs = [keep.tile([P, 2 * CW], U8, name="xs%d" % c, align_bytes=64) for c in range(CH)]
        vs = [keep.tile([P, CW], F32, name="vs%d" % c) for c in range(CH)]
        w1q = keep.tile([P, 1024], U32, name="w1q", align_bytes=64)
        w1s = keep.tile([P, 1024], U8, name="w1s", align_bytes=64)
        w2q = keep.tile([P, 512], U32, name="w2q", align_bytes=64)
        w2s = keep.tile([P, 512], U8, name="w2s", align_bytes=64)
        ident = keep.tile([P, P], F32, name="ident")
        b1f = keep.tile([P, 4], F32, name="b1f")
        b2f = keep.tile([P, 4], F32, name="b2f")
        acc1 = keep.tile([P, 32], F32, name="acc1")
        acc2 = keep.tile([P, 32], F32, name="acc2")
        sx = keep.tile([P, NT], F32, name="sx")
        sh = keep.tile([P, NT], F32, name="sh")
        sv = keep.tile([P, NT], F32, name="sv")
        k1 = keep.tile([P, 1], F32, name="k1")
        cm1 = keep.tile([P, 4], F32, name="cm1")
        s1 = keep.tile([P, 4], F32, name="s1")
        s2 = keep.tile([P, 4], F32, name="s2")
        jx = keep.tile([P, D0], BF16, name="jx")
        ja = keep.tile([P, CW], BF16, name="ja")
        j8 = keep.tile([P, 8], F32, name="j8")
        cm2b = keep.tile([P, D2], F32, name="cm2b")
        m2r = keep.tile([P, D2], F32, name="m2r")
        m1r = keep.tile([P, D1], F32, name="m1r")

        zeros = keep.tile([P, CW], F32, name="zeros")

        make_identity(nc, ident[:])
        nc.gpsimd.memset(zeros[:], 0.0)

        def spread_row_sums(c):
            sb = banks["pt"].tile([P, CW], F32, name="sb", tag="pt")
            for l in range(4):
                a = 4 * c + l
                nc.tensor.transpose(sb[:, l * P : (l + 1) * P], sx[:, a : a + 1].to_broadcast([P, P]), ident[:])
            return sb

        def relu_and_sum(on_vector, v, z, bias, acc, col):
            total = acc[:, col : col + 1]
            if on_vector:
                nc.vector.scalar_tensor_tensor(
                    out=v, in0=z[:], scalar=bias, in1=zeros[:], op0=ALU.add, op1=ALU.max, accum_out=total
                )
            else:
                nc.scalar.activation(out=v, in_=z[:], func=FN.Relu, bias=bias, scale=1.0, accum_out=total)

        def layer1(t, c, on_vector=False):
            z = banks["pz"].tile([P, CW], F32, name="z", tag="z")
            for g in range(2):
                wcols = slice(g * 512 + t * P, g * 512 + (t + 1) * P)
                xcols = slice(g * CW, (g + 1) * CW)
                nc.tensor.matmul_mx(
                    out=z[:],
                    lhsT=w1q[:, wcols].bitcast(FP8X4),
                    lhsT_scale=w1s[:, wcols],
                    rhs=xq[c][:, xcols].bitcast(FP8X4),
                    rhs_scale=xs[c][:, xcols],
                    start=(g == 0),
                    stop=(g == 1),
                )
            relu_and_sum(on_vector, hv[c][:, t * CW : (t + 1) * CW], z, b1f[:, t : t + 1], acc1, t * CH + c)

        def add_v1(c):
            nc.gpsimd.tensor_tensor(out=vs[c][:], in0=hv[c][:, 0:CW], in1=hv[c][:, CW : 2 * CW], op=ALU.add)
            nc.gpsimd.tensor_tensor(out=vs[c][:], in0=vs[c][:], in1=hv[c][:, 2 * CW : 3 * CW], op=ALU.add)

        def scaled_mean1(t):
            nc.vector.tensor_scalar(
                out=j8[:],
                in0=acc1[:, t * CH : (t + 1) * CH],
                scalar1=C / ROWS,
                scalar2=None,
                op0=ALU.mult,
                op1=ALU.add,
                accum_out=cm1[:, t : t + 1],
            )

        sbs = {}
        with tc.tile_pool(name="stage", bufs=1) as stage, ExitStack() as first_banks:
            banks["pt"] = first_banks.enter_context(tc.psum_pool(name="pt", bufs=4))
            banks["pz"] = first_banks.enter_context(tc.psum_pool(name="pz", bufs=4))
            xn = {}
            xg = {}

            def load_x(c, pieces):
                xt = stage.tile([P, 4 * D0], BF16, name="xn", tag="xn", bufs=5)
                n = 4 * D0 // pieces
                for i in range(pieces):
                    nc.sync.dma_start(
                        out=xt[:, i * n : (i + 1) * n], in_=x_v[:, c * 4 * D0 + i * n : c * 4 * D0 + (i + 1) * n]
                    )
                xn[c] = xt

            def words_to_k(words, first, grouped, col0, on_vector):
                bank = banks["pt"].tile([P, CW], F32, name="xt", tag="pt")
                for g in range(2):
                    for u in range(2):
                        b = 2 * g + u
                        w0 = first + g * 2 * P + u
                        nc.tensor.transpose(
                            bank[:, b * P : (b + 1) * P], words[:, w0 : first + (g + 1) * 2 * P : 2], ident[:]
                        )
                dst = grouped[:].bitcast(F32).rearrange("q (g c u) -> q g c u", g=2, u=2)[:, :, col0 : col0 + P, :]
                src = bank[:].rearrange("q (g u c) -> q g c u", g=2, u=2)
                if on_vector:
                    nc.vector.tensor_copy(out=dst, in_=src)
                else:
                    nc.scalar.copy(out=dst, in_=src)

            def transpose_x(c):
                xg[c] = stage.tile([P, 4 * D0], BF16, name="xg", tag="xg", bufs=2, align_bytes=64)
                for l in range(4):
                    words_to_k(xn[c][:].bitcast(F32), l * 512, xg[c], l * P, False)

            def row_sums_x(c):
                for l in range(4):
                    a = 4 * c + l
                    row = xn[c][:, l * D0 : (l + 1) * D0]
                    nc.vector.tensor_scalar(
                        out=jx[:],
                        in0=row,
                        scalar1=1.0,
                        scalar2=None,
                        op0=ALU.mult,
                        op1=ALU.add,
                        accum_out=sx[:, a : a + 1],
                    )

            def quantise_x(c):
                nc.vector.quantize_mx(out=xq[c][:].bitcast(FP8X4), scales=xs[c][:], in_=xg[c][:])

            def prepare_w2():
                w2words = w2n[:].bitcast(F32).rearrange("p (t w u) -> p t u w", t=4, u=2)
                w2gw = w2g[:].bitcast(F32).rearrange("q (t c u) -> q t c u", t=4, u=2)
                for h in range(2):
                    bank = banks["pt"].tile([P, CW], F32, name="w2t", tag="pt")
                    for tl in range(2):
                        for u in range(2):
                            k = tl * 2 + u
                            nc.tensor.transpose(
                                bank[:, k * P : (k + 1) * P], w2words[:, 2 * h + tl, u, :], ident[:]
                            )
                    nc.scalar.copy(
                        out=w2gw[:, 2 * h : 2 * h + 2, :, :],
                        in_=bank[:].rearrange("q (t u c) -> q t c u", t=2, u=2),
                    )
                bank = banks["pt"].tile([P, CW], F32, name="b2t", tag="pt")
                nc.tensor.transpose(bank[:, 0:P], b2pad[:], ident[:])
                nc.vector.tensor_copy(out=b2f[:], in_=bank[:, 0:4])
                nc.vector.quantize_mx(out=w2q[:].bitcast(FP8X4), scales=w2s[:], in_=w2g[:])

            w1n = stage.tile([P, 4 * D0], BF16, name="w1n")
            w1g = stage.tile([P, 4 * D0], BF16, name="w1g", align_bytes=64)
            w2n = stage.tile([P, 4 * D1], BF16, name="w2n")
            w2g = stage.tile([P, 4 * D1], BF16, name="w2g", align_bytes=64)
            b1r = stage.tile([P, 4], BF16, name="b1r")
            b2r = stage.tile([4, P], BF16, name="b2r")
            b2pad = stage.tile([P, P], F32, name="b2pad")

            nc.sync.dma_start(out=b1r[:], in_=b1.rearrange("(p t) -> p t", t=4))
            nc.sync.dma_start(out=b2r[:], in_=b2.rearrange("(t p) -> t p", p=P))
            load_x(0, 4)
            for t in range(4):
                nc.sync.dma_start(
                    out=w1n[:, t * D0 : (t + 1) * D0], in_=W1.rearrange("(p t) i -> p (t i)", t=4)[:, t * D0 : (t + 1) * D0]
                )
            for c in range(1, 5):
                load_x(c, 1)
            nc.sync.dma_start(
                out=w2n[:].rearrange("p (t o) -> p t o", t=4), in_=W2.rearrange("(t p) o -> p t o", p=P)
            )

            transpose_x(0)
            row_sums_x(0)
            nc.vector.tensor_copy(out=b1f[:], in_=b1r[:])
            nc.vector.memset(b2pad[:], 0.0)
            nc.vector.tensor_copy(out=b2pad[0:4, :], in_=b2r[:])
            quantise_x(0)
            for t in range(4):
                words_to_k(w1n[:].bitcast(F32), t * 512, w1g, t * P, t in (1, 3))
            transpose_x(1)
            nc.vector.quantize_mx(out=w1q[:].bitcast(FP8X4), scales=w1s[:], in_=w1g[:])

            for c in range(CH):
                if c + 5 < CH:
                    load_x(c + 5, 1)
                for t in range(3):
                    layer1(t, c)
                add_v1(c)
                if c + 1 < CH:
                    quantise_x(c + 1)
                if c + 2 < CH:
                    transpose_x(c + 2)
                if c + 1 < CH:
                    row_sums_x(c + 1)
                if c == 6:
                    prepare_w2()

        work = ctx.enter_context(tc.tile_pool(name="work", bufs=1))
        banks["pt"] = ctx.enter_context(tc.psum_pool(name="ps", bufs=3))
        banks["pz"] = ctx.enter_context(tc.psum_pool(name="pm", bufs=4))
        banks["pv"] = ctx.enter_context(tc.psum_pool(name="pv", bufs=1))
        for c in range(3):
            sbs[c] = spread_row_sums(c)
        hq = {}
        hs = {}
        ht = {}
        hg = {}
        v2 = {}

        def correct(t, c):
            if t == 0:
                ht[c] = work.tile([P, 4 * CW], BF16, name="ht", tag="ht", bufs=5)
            seg = slice(t * CW, (t + 1) * CW)
            nc.vector.scalar_tensor_tensor(
                out=ht[c][:, seg],
                in0=sbs[c][:],
                scalar=cm1[:, t : t + 1],
                in1=hv[c][:, seg],
                op0=ALU.mult,
                op1=ALU.add,
            )

        def row_sums_v1(c):
            bank = banks["pv"].tile([P, CW], F32, name="svb", tag="v")
            for l in range(4):
                for k, part in enumerate((vs[c][:, l * P : (l + 1) * P], hv[c][:, 3 * CW + l * P : 3 * CW + (l + 1) * P])):
                    nc.tensor.matmul(
                        out=bank[:, l * P : (l + 1) * P],
                        lhsT=part,
                        rhs=ident[:],
                        is_transpose=True,
                        start=(k == 0),
                        stop=(k == 1),
                    )
            for l in range(4):
                a = 4 * c + l
                nc.scalar.activation(
                    out=ja[:, 0:P], in_=bank[:, l * P : (l + 1) * P], func=FN.Copy, accum_out=sv[:, a : a + 1]
                )

        def regroup(c):
            hg[c] = work.tile([P, 4 * CW], BF16, name="hg", tag="hg", bufs=3, align_bytes=64)
            dst = hg[c][:].rearrange("p (c i t) -> p c t i", i=4, t=4)
            src = ht[c][:].rearrange("p (t c i) -> p c t i", t=4, i=4)
            if c in (0, 1, CH - 1):
                nc.vector.tensor_copy(out=dst, in_=src)
            else:
                whole = hg[c][:].rearrange("p (c t) -> p c t", t=4)
                tiles = ht[c][:].rearrange("p (t c) -> p c t", t=4)
                for i in range(4):
                    part = slice(i * P, (i + 1) * P)
                    nc.gpsimd.tensor_scalar(
                        out=whole[:, part, :],
                        in0=tiles[:, part, :],
                        scalar1=1.0,
                        scalar2=0.0,
                        op0=ALU.mult,
                        op1=ALU.add,
                    )

        def quantise_h(c):
            hq[c] = work.tile([P, CW], U32, name="hq", tag="hq", bufs=3, align_bytes=64)
            hs[c] = work.tile([P, CW], U8, name="hs", tag="hs", bufs=3, align_bytes=64)
            nc.vector.quantize_mx(out=hq[c][:].bitcast(FP8X4), scales=hs[c][:], in_=hg[c][:])

        def product2(t, c, in_ps=False):
            pool, tag = (banks["pt"], "pt") if in_ps else (banks["pz"], "z")
            z = pool.tile([P, CW], F32, name="z2", tag=tag)
            nc.tensor.matmul_mx(
                out=z[:],
                lhsT=w2q[:, t * P : (t + 1) * P].bitcast(FP8X4),
                lhsT_scale=w2s[:, t * P : (t + 1) * P],
                rhs=hq[c][:].bitcast(FP8X4),
                rhs_scale=hs[c][:],
                start=True,
                stop=True,
            )
            return z

        def exit2(t, c, z, on_vector=False):
            relu_and_sum(on_vector, v2[c][:, t * CW : (t + 1) * CW], z, b2f[:, t : t + 1], acc2, t * CH + c)

        def sum_of_means():
            kb = banks["pz"].tile([P, CW], F32, name="kb", tag="z")
            for t in range(4):
                nc.tensor.transpose(kb[:, t * P : (t + 1) * P], cm1[:, t : t + 1].to_broadcast([P, P]), ident[:])
            nc.scalar.activation(out=ja[:], in_=kb[:], func=FN.Copy, accum_out=k1[:, 0:1])

        def store_m1():
            nc.vector.tensor_reduce(
                out=s1[:], in_=acc1[:].rearrange("p (t c) -> p t c", t=4), axis=AXIS.X, op=ALU.add
            )
            m1b = banks["pz"].tile([P, CW], F32, name="m1b", tag="z")
            for t in range(4):
                nc.tensor.transpose(m1b[:, t * P : (t + 1) * P], s1[:, t : t + 1].to_broadcast([P, P]), ident[:])
            nc.scalar.activation(
                out=m1r[0:32, :].rearrange("p (k t) -> p k t", t=4),
                in_=m1b[0:32, :].rearrange("p (t k) -> p k t", t=4),
                func=FN.Copy,
                scale=1.0 / ROWS,
            )
            nc.sync.dma_start(out=out_1.rearrange("(o n) -> o n", o=1), in_=m1r[0:1, :])

        def new_v2(c):
            if c < EARLY:
                v2[c] = keep.tile([P, 4 * CW], F32, name="v2_%d" % c, tag="hv%d" % c)
            else:
                v2[c] = work.tile([P, 4 * CW], F32, name="v2_%d" % c)

        def row_sums_h(first, last):
            cols = slice(4 * first, 4 * last)
            nc.vector.scalar_tensor_tensor(
                out=sh[:, cols], in0=sx[:, cols], scalar=k1[:, 0:1], in1=sv[:, cols], op0=ALU.mult, op1=ALU.add
            )

        def natural(a):
            pool, tag = (banks["pt"], "pt") if a >= 3 and (a - 3) % 7 < 3 else (banks["pz"], "z")
            bank = pool.tile([P, CW], F32, name="vn", tag=tag)
            for t in range(4):
                first = t * CW + (a % 4) * P
                nc.tensor.transpose(bank[:, t * P : (t + 1) * P], v2[a // 4][:, first : first + P], ident[:])
            return bank

        LEAD = 3
        for t in range(3):
            scaled_mean1(t)
        for c in range(CH):
            layer1(3, c)
        for c in range(LEAD):
            for t in range(3):
                correct(t, c)
        scaled_mean1(3)
        for c in range(CH):
            for t in range(3 if c < LEAD else 0, 4):
                correct(t, c)
            if c < EARLY:
                row_sums_v1(c)
            if c + 3 < CH:
                sbs[c + 3] = spread_row_sums(c + 3)
            if c >= 1:
                quantise_h(c - 1)
            regroup(c)
            if c >= 1:
                new_v2(c - 1)
                for t in range(4):
                    exit2(t, c - 1, product2(t, c - 1))
            if c == 2:
                sum_of_means()
            if c == 3:
                store_m1()
        vn = {}
        nc.vector.tensor_reduce(
            out=s2[:],
            in_=acc2[:].rearrange("p (t c) -> p t c", t=4)[:, :, 0 : CH - 2],
            axis=AXIS.X,
            op=ALU.add,
        )
        quantise_h(CH - 1)
        new_v2(CH - 1)
        last = [product2(t, CH - 1, t < 3) for t in range(4)]
        for a in range(3):
            vn[a] = natural(a)
        for t in range(4):
            exit2(t, CH - 1, last[t], t in (0, 1, 2))

        row_sums_h(0, EARLY)
        AHEAD = 6
        mb = banks["pv"].tile([P, CW], F32, name="mb", tag="v")
        for t in range(4):
            n = t * CH + CH
            for k, part in enumerate((s2[:, t : t + 1], acc2[:, n - 2 : n - 1], acc2[:, n - 1 : n])):
                nc.tensor.matmul(
                    out=mb[:, t * P : (t + 1) * P],
                    lhsT=part.to_broadcast([P, P]),
                    rhs=ident[:],
                    is_transpose=True,
                    start=(k == 0),
                    stop=(k == 2),
                )
        nc.scalar.activation(out=cm2b[:, 0:256], in_=mb[:, 0:256], func=FN.Copy, scale=C / ROWS)
        nc.vector.tensor_scalar(out=cm2b[:, 256:512], in0=mb[:, 256:512], scalar1=C / ROWS, scalar2=None, op0=ALU.mult)
        nc.scalar.activation(out=m2r[0:32, :], in_=mb[0:32, :], func=FN.Copy, scale=1.0 / ROWS)
        nc.sync.dma_start(out=out_2.rearrange("(o n) -> o n", o=1), in_=m2r[0:1, :])
        for a in range(3, AHEAD):
            vn[a] = natural(a)

        ob = None
        for a in range(NT):
            if a % 2 == 0:
                ob = work.tile([P, 2 * D2], F32, name="ob", tag="ob", bufs=8)
            if a % 4 == 0 and a >= 4 * EARLY:
                row_sums_h(a // 4, a // 4 + 1)
            nc.vector.scalar_tensor_tensor(
                out=ob[:, (a % 2) * D2 : (a % 2 + 1) * D2],
                in0=cm2b[:],
                scalar=sh[:, a : a + 1],
                in1=vn[a][:],
                op0=ALU.mult,
                op1=ALU.add,
            )
            if a % 2 == 1:
                nc.sync.dma_start(out=out_v[:, (a - 1) * D2 : (a + 1) * D2], in_=ob[:])
            if a + AHEAD < NT:
                vn[a + AHEAD] = natural(a + AHEAD)
            if a % 4 == 2 and a < 4 * (CH - EARLY):
                row_sums_v1(EARLY + a // 4)
